import numpy as np
import ml_dtypes


def mxq(x, axis, fmt="e4m3"):
    dtype, down = {"e4m3": (ml_dtypes.float8_e4m3fn, 7), "e5m2": (ml_dtypes.float8_e5m2, 14)}[fmt]
    v = np.moveaxis(np.asarray(x, np.float32).astype(ml_dtypes.bfloat16).astype(np.float64), axis, -1)
    blocks = v.reshape(v.shape[:-1] + (-1, 32))
    amax = np.abs(blocks).max(-1, keepdims=True)
    byte = np.maximum(np.where(amax > 0, np.frexp(amax)[1] - 1 + 127, 0) - down, 1)
    scale = np.exp2(byte - 127.0)
    codes = (blocks / scale).astype(np.float32).astype(dtype).astype(np.float64)
    return np.moveaxis((codes * scale).reshape(v.shape), -1, axis)


WIDE = False


def mx_kscale(k):
    if not WIDE:
        return np.ones(k)
    levels = np.array([10, -10, 5, -5, 0])
    a = np.random.permutation(np.resize(levels, k // 512 * 4)).reshape(k // 512, 4)
    idx = np.arange(k)
    return np.exp2(a[idx // 512, idx % 128 // 32])


BF16 = ml_dtypes.bfloat16


def bf(x):
    return np.asarray(x, np.float32).astype(BF16)


def f64(x):
    return np.asarray(x).astype(np.float64)


E2M1 = np.array([0.0, 0.5, 1.0, 1.5, 2.0, 3.0, 4.0, 6.0, -0.0, -0.5, -1.0, -1.5, -2.0, -3.0, -4.0, -6.0])


def pack_weight(w, fmt):
    k, n = w.shape
    w = f64(bf(w)).reshape(k // 32, 32, n)
    amax = np.abs(w).max(1)
    if fmt == "e4m3":
        byte = np.frexp(amax)[1] - 1 + 127 - 7
    else:
        mant, ex = np.frexp(amax / 6.0)
        byte = np.where(mant > 0.5, ex, ex - 1) + 127
    byte = np.clip(np.where(amax > 0, byte, 1), 1, 254)
    scaled = (w * np.exp2(127.0 - byte)[:, None, :]).reshape(k, n).astype(np.float32)
    by_word = np.ascontiguousarray(scaled.reshape(k // 512, 128, 4, n).transpose(0, 1, 3, 2))
    if fmt == "e4m3":
        words = by_word.astype(ml_dtypes.float8_e4m3fn).view(np.uint8)
    else:
        c = by_word.astype(ml_dtypes.float4_e2m1fn).view(np.uint8) & 0xF
        words = c[..., 0::2] | (c[..., 1::2] << 4)
    return np.ascontiguousarray(words), np.ascontiguousarray(byte.astype(np.uint8).reshape(k // 512, 16, n))


def unpack_weight(words, scales, fmt):
    g, p, n, _ = words.shape
    if fmt == "e4m3":
        vals = np.ascontiguousarray(words).view(ml_dtypes.float8_e4m3fn).astype(np.float64)
    else:
        nib = np.empty((g, p, n, 4), np.uint8)
        nib[..., 0::2] = words & 0xF
        nib[..., 1::2] = words >> 4
        vals = E2M1[nib]
    vals = vals * np.repeat(np.exp2(scales.astype(np.float64) - 127.0), 8, axis=1)[..., None]
    return vals.transpose(0, 1, 3, 2).reshape(g * 512, n)


B, G, Z1, Z2, H, PD = 4096, 4, 256, 256, 512, 128


def glin(x, W_words, W_scales, cout, b):
    y = mxq(x, 2, "e4m3").transpose(1, 0, 2) @ unpack_weight(W_words, W_scales, "e4m3").reshape(G, H, cout)
    return y.transpose(1, 0, 2) + f64(b)


def setup_inputs():
    s = mx_kscale(H)
    h = np.maximum(np.random.standard_normal((B, G, H)), 0.0) + np.maximum(np.random.standard_normal((B, G, H)), 0.0)
    W3 = np.random.standard_normal((G, H, H)) / np.sqrt(H) * s[None, :, None] / s[None, None, :]
    b3 = bf(np.random.standard_normal((G, H)) * 0.2 * s)
    Wo = np.random.standard_normal((G, PD, H)) * 0.6 / np.sqrt(H) / s[None, None, :]
    bo = bf(np.random.standard_normal((G, PD)) * 0.2)
    W3_words, W3_scales = pack_weight(W3.swapaxes(1, 2).reshape(-1, H), "e4m3")
    Wo_words, Wo_scales = pack_weight(Wo.swapaxes(1, 2).reshape(-1, PD), "e4m3")
    return {"h": bf(h * s),
            "W3_words": W3_words,
            "W3_scales": W3_scales,
            "b3": b3,
            "Wo_words": Wo_words,
            "Wo_scales": Wo_scales,
            "bo": bo}


def reference(h, W3_words, W3_scales, b3, Wo_words, Wo_scales, bo):
    h = f64(h)
    h3 = np.maximum(glin(h, W3_words, W3_scales, H, b3), 0.0) + h
    out = glin(h3, Wo_words, Wo_scales, PD, bo)
    return out.reshape(B, G * PD)

@@ -1,0 +1,164 @@
+from contextlib import ExitStack
+
+from concourse import mybir
+from concourse.masks import make_identity
+
+F32 = mybir.dt.float32
+BF16 = mybir.dt.bfloat16
+I32 = mybir.dt.int32
+U32 = mybir.dt.uint32
+U8 = mybir.dt.uint8
+FP8X4 = mybir.dt.float8_e4m3fn_x4
+RELU = mybir.ActivationFunctionType.Relu
+ADD = mybir.AluOpType.add
+
+P = 128
+PACK = 4
+TOKENS = 4096
+CODES = 4
+HID = 512
+OUT = 128
+TILES = TOKENS // P
+CHUNK = 4
+
+FLOPS = 2 * TOKENS * CODES * HID * (HID + OUT)
+
+
+def tile_linearwdecoder_pb_t_e_kernel(tc, h, W3_words, W3_scales, b3, Wo_words, Wo_scales, bo, out):
+    nc = tc.nc
+    h_view = h.rearrange("(p i) g k -> p i (g k)", i=TILES)
+    out_view = out.rearrange("(p i) n -> p i n", i=TILES)
+
+    with ExitStack() as stack:
+        keep = stack.enter_context(tc.tile_pool(name="keep", bufs=1))
+        h_pool = stack.enter_context(tc.tile_pool(name="h_pool", bufs=TILES // CHUNK))
+        work = stack.enter_context(tc.tile_pool(name="work", bufs=3))
+        ps_t = stack.enter_context(tc.psum_pool(name="ps_t", bufs=2))
+        ps_x = stack.enter_context(tc.psum_pool(name="ps_x", bufs=2))
+        ps_z = stack.enter_context(tc.psum_pool(name="ps_z", bufs=3))
+        ps_o = stack.enter_context(tc.psum_pool(name="ps_o", bufs=1))
+
+        w3_scales = keep.tile([P, CODES, HID], U8, align_bytes=64)
+        wo_scales = keep.tile([P, CODES, OUT], U8, align_bytes=64)
+        nc.vector.memset(w3_scales[:].rearrange("p g n -> p (g n)").bitcast(I32), 0)
+        nc.vector.memset(wo_scales[:].rearrange("p g n -> p (g n)").bitcast(I32), 0)
+        for quad in range(4):
+            rows = slice(4 * quad, 4 * quad + 4)
+            live = slice(32 * quad, 32 * quad + 4)
+            nc.sync.dma_start(
+                out=w3_scales[live, :, :].bitcast(I32),
+                in_=W3_scales[:, rows, :].rearrange("g r n -> r g n").bitcast(I32),
+            )
+            nc.sync.dma_start(
+                out=wo_scales[live, :, :].bitcast(I32),
+                in_=Wo_scales[:, rows, :].rearrange("g r n -> r g n").bitcast(I32),
+            )
+
+        h_chunks = []
+        first = h_pool.tile([P, CHUNK, CODES * HID], BF16, name="h_chunk")
+        nc.sync.dma_start(out=first[:], in_=h_view[:, 0:CHUNK, :])
+        h_chunks.append(first)
+
+        w3_words = keep.tile([P, CODES, HID], U32, align_bytes=64)
+        nc.sync.dma_start(out=w3_words[:].bitcast(I32), in_=W3_words.rearrange("g p n t -> p g (n t)").bitcast(I32))
+        wo_words = keep.tile([P, CODES, OUT], U32, align_bytes=64)
+        nc.sync.dma_start(out=wo_words[:].bitcast(I32), in_=Wo_words.rearrange("g p n t -> p g (n t)").bitcast(I32))
+
+        for c in range(1, TILES // CHUNK):
+            chunk = h_pool.tile([P, CHUNK, CODES * HID], BF16, name="h_chunk")
+            nc.sync.dma_start(out=chunk[:], in_=h_view[:, c * CHUNK : (c + 1) * CHUNK, :])
+            h_chunks.append(chunk)
+
+        ident = keep.tile([P, P], F32)
+        make_identity(nc, ident[:])
+
+        bo_all = keep.tile([P, CODES * OUT], BF16)
+        nc.scalar.dma_start(out=bo_all[:], in_=bo.rearrange("g o -> (g o)").partition_broadcast(P))
+        b3_rows = keep.tile([P, HID], BF16)
+        nc.vector.memset(b3_rows[:], 0.0)
+        nc.scalar.dma_start(out=b3_rows[0:CODES, :], in_=b3)
+        b3_sorted = keep.tile([P, PACK, P], F32)
+        nc.vector.tensor_copy(out=b3_sorted[:], in_=b3_rows[:].rearrange("r (p t) -> r t p", t=PACK))
+        b3_t = ps_z.tile([P, PACK, P], F32, name="z")
+        for t in range(PACK):
+            nc.tensor.transpose(b3_t[:, t, :], b3_sorted[:, t, :], ident[:])
+        b3_cols = keep.tile([P, CODES * PACK], F32)
+        nc.vector.tensor_copy(
+            out=b3_cols[:].rearrange("p (g t) -> p g t", t=PACK),
+            in_=b3_t[:, :, 0:CODES].rearrange("p t g -> p g t"),
+        )
+
+        for i in range(TILES):
+            h_tile = h_chunks[i // CHUNK][:, i % CHUNK, :]
+            h_pairs = h_tile.bitcast(F32)
+
+            h_t = work.tile([P, CODES, P, PACK], BF16, align_bytes=64)
+            h_t_pairs = h_t[:].bitcast(F32)
+            for half in range(2):
+                tp = ps_t.tile([P, 2, 2, P], F32)
+                for gg in range(2):
+                    g = 2 * half + gg
+                    for u in range(2):
+                        nc.tensor.transpose(
+                            tp[:, gg, u, :], h_pairs[:, 256 * g + u : 256 * (g + 1) : 2], ident[:]
+                        )
+                nc.vector.tensor_copy(
+                    out=h_t_pairs[:, 2 * half : 2 * half + 2, :, :], in_=tp[:].rearrange("p g u w -> p g w u")
+                )
+            h_codes = work.tile([P, CODES * P], U32, align_bytes=64)
+            h_scales = work.tile([P, CODES * P], U8, align_bytes=64)
+            nc.vector.quantize_mx(
+                out=h_codes[:].bitcast(FP8X4), scales=h_scales[:], in_=h_t[:].rearrange("p g w t -> p (g w t)")
+            )
+
+            h3_t = work.tile([P, CODES, P, PACK], BF16, align_bytes=64)
+            for g in range(CODES):
+                cols = slice(g * P, (g + 1) * P)
+                x = ps_x.tile([P, HID], F32)
+                nc.tensor.matmul_mx(
+                    out=x[:],
+                    lhsT=h_codes[:, cols].bitcast(FP8X4),
+                    lhsT_scale=h_scales[:, cols],
+                    rhs=w3_words[:, g, :].bitcast(FP8X4),
+                    rhs_scale=w3_scales[:, g, :],
+                    start=True,
+                    stop=True,
+                )
+                x_sorted = work.tile([P, PACK, P], F32)
+                nc.scalar.copy(out=x_sorted[:], in_=x[:].rearrange("w (p t) -> w t p", t=PACK))
+                z = ps_z.tile([P, PACK, P], F32)
+                for t in range(PACK):
+                    nc.tensor.transpose(z[:, t, :], x_sorted[:, t, :], ident[:])
+                r = work.tile([P, PACK, P], F32)
+                for t in range(PACK):
+                    nc.scalar.activation(
+                        out=r[:, t, :],
+                        in_=z[:, t, :],
+                        func=RELU,
+                        bias=b3_cols[:, PACK * g + t : PACK * g + t + 1],
+                        scale=1.0,
+                    )
+                nc.vector.tensor_tensor(
+                    out=h3_t[:, g, :, :], in0=r[:].rearrange("p t w -> p w t"), in1=h_t[:, g, :, :], op=ADD
+                )
+            h3_codes = work.tile([P, CODES * P], U32, align_bytes=64)
+            h3_scales = work.tile([P, CODES * P], U8, align_bytes=64)
+            nc.vector.quantize_mx(
+                out=h3_codes[:].bitcast(FP8X4), scales=h3_scales[:], in_=h3_t[:].rearrange("p g w t -> p (g w t)")
+            )
+
+            o = ps_o.tile([P, CODES * OUT], F32)
+            for g in range(CODES):
+                cols = slice(g * P, (g + 1) * P)
+                nc.tensor.matmul_mx(
+                    out=o[:, g * OUT : (g + 1) * OUT],
+                    lhsT=h3_codes[:, cols].bitcast(FP8X4),
+                    lhsT_scale=h3_scales[:, cols],
+                    rhs=wo_words[:, g, :].bitcast(FP8X4),
+                    rhs_scale=wo_scales[:, g, :],
+                    start=True,
+                    stop=True,
+                )
+            o_sb = work.tile([P, CODES * OUT], F32)
+            nc.vector.tensor_tensor(out=o_sb[:], in0=o[:], in1=bo_all[:], op=ADD)
+            nc.sync.dma_start(out=out_view[:, i, :], in_=o_sb[:])

@@ -19,7 +19,10 @@ CODES = 4
 HID = 512
 OUT = 128
 TILES = TOKENS // P
-CHUNK = 4
+PAIR = 2
+W = PAIR * P
+PAIRS = TILES // PAIR
+UNITS = PAIRS * CODES
 
 FLOPS = 2 * TOKENS * CODES * HID * (HID + OUT)
 
@@ -31,12 +34,16 @@ def tile_linearwdecoder_pb_t_e_kernel(tc, h, W3_words, W3_scales, b3, Wo_words, 
 
     with ExitStack() as stack:
         keep = stack.enter_context(tc.tile_pool(name="keep", bufs=1))
-        h_pool = stack.enter_context(tc.tile_pool(name="h_pool", bufs=TILES // CHUNK))
-        work = stack.enter_context(tc.tile_pool(name="work", bufs=3))
-        ps_t = stack.enter_context(tc.psum_pool(name="ps_t", bufs=2))
-        ps_x = stack.enter_context(tc.psum_pool(name="ps_x", bufs=2))
-        ps_z = stack.enter_context(tc.psum_pool(name="ps_z", bufs=3))
-        ps_o = stack.enter_context(tc.psum_pool(name="ps_o", bufs=1))
+        h_pool = stack.enter_context(tc.tile_pool(name="h_pool", bufs=PAIRS))
+        two = stack.enter_context(tc.tile_pool(name="two", bufs=2))
+        four = stack.enter_context(tc.tile_pool(name="four", bufs=4))
+        ps_one = stack.enter_context(tc.psum_pool(name="ps_one", bufs=1))
+        ps_two = stack.enter_context(tc.psum_pool(name="ps_two", bufs=2))
+
+        h_pairs = []
+        for j in range(PAIRS):
+            h_pairs.append(h_pool.tile([P, PAIR, CODES * HID], BF16, name="h_pair"))
+        nc.sync.dma_start(out=h_pairs[0][:], in_=h_view[:, 0:PAIR, :])
 
         w3_scales = keep.tile([P, CODES, HID], U8, align_bytes=64)
         wo_scales = keep.tile([P, CODES, OUT], U8, align_bytes=64)
@@ -53,33 +60,27 @@ def tile_linearwdecoder_pb_t_e_kernel(tc, h, W3_words, W3_scales, b3, Wo_words, 
                 out=wo_scales[live, :, :].bitcast(I32),
                 in_=Wo_scales[:, rows, :].rearrange("g r n -> r g n").bitcast(I32),
             )
-
-        h_chunks = []
-        first = h_pool.tile([P, CHUNK, CODES * HID], BF16, name="h_chunk")
-        nc.sync.dma_start(out=first[:], in_=h_view[:, 0:CHUNK, :])
-        h_chunks.append(first)
-
         w3_words = keep.tile([P, CODES, HID], U32, align_bytes=64)
         nc.sync.dma_start(out=w3_words[:].bitcast(I32), in_=W3_words.rearrange("g p n t -> p g (n t)").bitcast(I32))
         wo_words = keep.tile([P, CODES, OUT], U32, align_bytes=64)
         nc.sync.dma_start(out=wo_words[:].bitcast(I32), in_=Wo_words.rearrange("g p n t -> p g (n t)").bitcast(I32))
-
-        for c in range(1, TILES // CHUNK):
-            chunk = h_pool.tile([P, CHUNK, CODES * HID], BF16, name="h_chunk")
-            nc.sync.dma_start(out=chunk[:], in_=h_view[:, c * CHUNK : (c + 1) * CHUNK, :])
-            h_chunks.append(chunk)
+        for j in range(1, PAIRS):
+            nc.sync.dma_start(out=h_pairs[j][:], in_=h_view[:, j * PAIR : (j + 1) * PAIR, :])
 
         ident = keep.tile([P, P], F32)
         make_identity(nc, ident[:])
 
-        bo_all = keep.tile([P, CODES * OUT], BF16)
-        nc.scalar.dma_start(out=bo_all[:], in_=bo.rearrange("g o -> (g o)").partition_broadcast(P))
+        bo_row = keep.tile([P, CODES * OUT], BF16)
+        nc.scalar.dma_start(out=bo_row[:], in_=bo.rearrange("g o -> (g o)").partition_broadcast(P))
+        bo_rep = keep.tile([P, PAIR, CODES * OUT], F32)
+        for s in range(PAIR):
+            nc.vector.tensor_copy(out=bo_rep[:, s, :], in_=bo_row[:])
         b3_rows = keep.tile([P, HID], BF16)
         nc.vector.memset(b3_rows[:], 0.0)
         nc.scalar.dma_start(out=b3_rows[0:CODES, :], in_=b3)
         b3_sorted = keep.tile([P, PACK, P], F32)
         nc.vector.tensor_copy(out=b3_sorted[:], in_=b3_rows[:].rearrange("r (p t) -> r t p", t=PACK))
-        b3_t = ps_z.tile([P, PACK, P], F32, name="z")
+        b3_t = ps_one.tile([P, PACK, P], F32, tag="o")
         for t in range(PACK):
             nc.tensor.transpose(b3_t[:, t, :], b3_sorted[:, t, :], ident[:])
         b3_cols = keep.tile([P, CODES * PACK], F32)
@@ -88,77 +89,133 @@ def tile_linearwdecoder_pb_t_e_kernel(tc, h, W3_words, W3_scales, b3, Wo_words, 
             in_=b3_t[:, :, 0:CODES].rearrange("p t g -> p g t"),
         )
 
-        for i in range(TILES):
-            h_tile = h_chunks[i // CHUNK][:, i % CHUNK, :]
-            h_pairs = h_tile.bitcast(F32)
+        tp_of, h_t_of, h_q_of, x_of, xs_of, z_of, r_of, h3_t_of, h3_q_of, o_of, o_sb_of = (
+            {}, {}, {}, {}, {}, {}, {}, {}, {}, {}, {},
+        )
 
-            h_t = work.tile([P, CODES, P, PACK], BF16, align_bytes=64)
-            h_t_pairs = h_t[:].bitcast(F32)
-            for half in range(2):
-                tp = ps_t.tile([P, 2, 2, P], F32)
-                for gg in range(2):
-                    g = 2 * half + gg
-                    for u in range(2):
-                        nc.tensor.transpose(
-                            tp[:, gg, u, :], h_pairs[:, 256 * g + u : 256 * (g + 1) : 2], ident[:]
-                        )
-                nc.vector.tensor_copy(
-                    out=h_t_pairs[:, 2 * half : 2 * half + 2, :, :], in_=tp[:].rearrange("p g u w -> p g w u")
-                )
-            h_codes = work.tile([P, CODES * P], U32, align_bytes=64)
-            h_scales = work.tile([P, CODES * P], U8, align_bytes=64)
+        def transpose_h(k):
+            j, g = divmod(k, CODES)
+            tp = ps_one.tile([P, 2, W], F32, name="tp")
+            for s in range(PAIR):
+                words = h_pairs[j][:, s, :].bitcast(F32)
+                for u in range(2):
+                    nc.tensor.transpose(
+                        tp[:, u, s * P : (s + 1) * P], words[:, 256 * g + u : 256 * (g + 1) : 2], ident[:]
+                    )
+            tp_of[k] = tp
+
+        def copy_h_t(k):
+            h_t = four.tile([P, W, PACK], BF16, align_bytes=64, name="h_t")
+            nc.vector.tensor_copy(out=h_t[:].bitcast(F32), in_=tp_of[k][:].rearrange("p u w -> p w u"))
+            h_t_of[k] = h_t
+
+        def quantise(values, name):
+            codes = two.tile([P, W], U32, align_bytes=64, name=name + "_codes")
+            scales = two.tile([P, W], U8, align_bytes=64, name=name + "_scales")
             nc.vector.quantize_mx(
-                out=h_codes[:].bitcast(FP8X4), scales=h_scales[:], in_=h_t[:].rearrange("p g w t -> p (g w t)")
+                out=codes[:].bitcast(FP8X4), scales=scales[:], in_=values[:].rearrange("p w t -> p (w t)")
             )
+            return codes, scales
 
-            h3_t = work.tile([P, CODES, P, PACK], BF16, align_bytes=64)
-            for g in range(CODES):
-                cols = slice(g * P, (g + 1) * P)
-                x = ps_x.tile([P, HID], F32)
+        def first_layer(k):
+            g = k % CODES
+            codes, scales = h_q_of[k]
+            x_of[k] = []
+            for s in range(PAIR):
+                cols = slice(s * P, (s + 1) * P)
+                x = ps_two.tile([P, HID], F32, name="x")
                 nc.tensor.matmul_mx(
                     out=x[:],
-                    lhsT=h_codes[:, cols].bitcast(FP8X4),
-                    lhsT_scale=h_scales[:, cols],
+                    lhsT=codes[:, cols].bitcast(FP8X4),
+                    lhsT_scale=scales[:, cols],
                     rhs=w3_words[:, g, :].bitcast(FP8X4),
                     rhs_scale=w3_scales[:, g, :],
                     start=True,
                     stop=True,
                 )
-                x_sorted = work.tile([P, PACK, P], F32)
-                nc.scalar.copy(out=x_sorted[:], in_=x[:].rearrange("w (p t) -> w t p", t=PACK))
-                z = ps_z.tile([P, PACK, P], F32)
-                for t in range(PACK):
-                    nc.tensor.transpose(z[:, t, :], x_sorted[:, t, :], ident[:])
-                r = work.tile([P, PACK, P], F32)
-                for t in range(PACK):
-                    nc.scalar.activation(
-                        out=r[:, t, :],
-                        in_=z[:, t, :],
-                        func=RELU,
-                        bias=b3_cols[:, PACK * g + t : PACK * g + t + 1],
-                        scale=1.0,
-                    )
-                nc.vector.tensor_tensor(
-                    out=h3_t[:, g, :, :], in0=r[:].rearrange("p t w -> p w t"), in1=h_t[:, g, :, :], op=ADD
-                )
-            h3_codes = work.tile([P, CODES * P], U32, align_bytes=64)
-            h3_scales = work.tile([P, CODES * P], U8, align_bytes=64)
-            nc.vector.quantize_mx(
-                out=h3_codes[:].bitcast(FP8X4), scales=h3_scales[:], in_=h3_t[:].rearrange("p g w t -> p (g w t)")
-            )
+                x_of[k].append(x)
 
-            o = ps_o.tile([P, CODES * OUT], F32)
-            for g in range(CODES):
-                cols = slice(g * P, (g + 1) * P)
+        def copy_x(k):
+            xs_of[k] = []
+            for s in range(PAIR):
+                x_sorted = four.tile([P, PACK, P], F32, name="x_sorted")
+                nc.scalar.copy(out=x_sorted[:], in_=x_of[k][s][:].rearrange("w (p t) -> w t p", t=PACK))
+                xs_of[k].append(x_sorted)
+
+        def transpose_x(k):
+            z = [ps_two.tile([P, 2, W], F32, name="z_lo"), ps_two.tile([P, 2, W], F32, name="z_hi")]
+            for s in range(PAIR):
+                for t in range(PACK):
+                    nc.tensor.transpose(z[t // 2][:, t % 2, s * P : (s + 1) * P], xs_of[k][s][:, t, :], ident[:])
+            z_of[k] = z
+
+        def bias_relu(k):
+            g = k % CODES
+            r = two.tile([P, PACK, W], F32, name="r")
+            for t in range(PACK):
+                nc.scalar.activation(
+                    out=r[:, t, :],
+                    in_=z_of[k][t // 2][:, t % 2, :],
+                    func=RELU,
+                    bias=b3_cols[:, PACK * g + t : PACK * g + t + 1],
+                    scale=1.0,
+                )
+            r_of[k] = r
+
+        def add_residual(k):
+            h3_t = two.tile([P, W, PACK], BF16, align_bytes=64, name="h3_t")
+            nc.vector.tensor_tensor(out=h3_t[:], in0=r_of[k][:].rearrange("p t w -> p w t"), in1=h_t_of[k][:], op=ADD)
+            h3_t_of[k] = h3_t
+
+        def second_layer(k):
+            g = k % CODES
+            codes, scales = h3_q_of[k]
+            o = ps_one.tile([P, PAIR, OUT], F32, name="o")
+            for s in range(PAIR):
+                cols = slice(s * P, (s + 1) * P)
                 nc.tensor.matmul_mx(
-                    out=o[:, g * OUT : (g + 1) * OUT],
-                    lhsT=h3_codes[:, cols].bitcast(FP8X4),
-                    lhsT_scale=h3_scales[:, cols],
+                    out=o[:, s, :],
+                    lhsT=codes[:, cols].bitcast(FP8X4),
+                    lhsT_scale=scales[:, cols],
                     rhs=wo_words[:, g, :].bitcast(FP8X4),
                     rhs_scale=wo_scales[:, g, :],
                     start=True,
                     stop=True,
                 )
-            o_sb = work.tile([P, CODES * OUT], F32)
-            nc.vector.tensor_tensor(out=o_sb[:], in0=o[:], in1=bo_all[:], op=ADD)
-            nc.sync.dma_start(out=out_view[:, i, :], in_=o_sb[:])
+            o_of[k] = o
+
+        def bias_store(k):
+            j, g = divmod(k, CODES)
+            if g == 0:
+                o_sb_of[j] = two.tile([P, PAIR, CODES * OUT], F32, name="o_sb")
+            cols = slice(g * OUT, (g + 1) * OUT)
+            nc.vector.tensor_tensor(out=o_sb_of[j][:, :, cols], in0=o_of[k][:], in1=bo_rep[:, :, cols], op=ADD)
+            if g == CODES - 1:
+                nc.sync.dma_start(out=out_view[:, j * PAIR : (j + 1) * PAIR, :], in_=o_sb_of[j][:])
+
+        def live(k):
+            return 0 <= k < UNITS
+
+        with tc.manual_schedule():
+            for k in range(-2, UNITS + 3):
+                if live(k):
+                    first_layer(k)
+                    copy_x(k)
+                if live(k - 3):
+                    second_layer(k - 3)
+                if live(k + 2):
+                    transpose_h(k + 2)
+                if live(k):
+                    transpose_x(k)
+                if live(k - 1):
+                    bias_relu(k - 1)
+                if live(k + 1):
+                    copy_h_t(k + 1)
+                if live(k - 2):
+                    add_residual(k - 2)
+                if live(k + 1):
+                    h_q_of[k + 1] = quantise(h_t_of[k + 1], "h")
+                if live(k - 2):
+                    h3_q_of[k - 2] = quantise(h3_t_of[k - 2], "h3")
+                if live(k - 3):
+                    bias_store(k - 3)

@@ -23,6 +23,7 @@ PAIR = 2
 W = PAIR * P
 PAIRS = TILES // PAIR
 UNITS = PAIRS * CODES
+GPSIMD_TOKENS = 128
 
 FLOPS = 2 * TOKENS * CODES * HID * (HID + OUT)
 
@@ -164,7 +165,14 @@ def tile_linearwdecoder_pb_t_e_kernel(tc, h, W3_words, W3_scales, b3, Wo_words, 
 
         def add_residual(k):
             h3_t = two.tile([P, W, PACK], BF16, align_bytes=64, name="h3_t")
-            nc.vector.tensor_tensor(out=h3_t[:], in0=r_of[k][:].rearrange("p t w -> p w t"), in1=h_t_of[k][:], op=ADD)
+            r_by_token = r_of[k][:].rearrange("p t w -> p w t")
+            cut = W - GPSIMD_TOKENS
+            nc.vector.tensor_tensor(
+                out=h3_t[:, 0:cut, :], in0=r_by_token[:, 0:cut, :], in1=h_t_of[k][:, 0:cut, :], op=ADD
+            )
+            nc.gpsimd.tensor_tensor(
+                out=h3_t[:, cut:W, :], in0=r_by_token[:, cut:W, :], in1=h_t_of[k][:, cut:W, :], op=ADD
+            )
             h3_t_of[k] = h3_t
 
         def second_layer(k):
@@ -197,12 +205,12 @@ def tile_linearwdecoder_pb_t_e_kernel(tc, h, W3_words, W3_scales, b3, Wo_words, 
             return 0 <= k < UNITS
 
         with tc.manual_schedule():
-            for k in range(-2, UNITS + 3):
+            for k in range(-2, UNITS + 4):
                 if live(k):
                     first_layer(k)
                     copy_x(k)
-                if live(k - 3):
-                    second_layer(k - 3)
+                if live(k - 4):
+                    second_layer(k - 4)
                 if live(k + 2):
                     transpose_h(k + 2)
                 if live(k):
@@ -215,7 +223,7 @@ def tile_linearwdecoder_pb_t_e_kernel(tc, h, W3_words, W3_scales, b3, Wo_words, 
                     add_residual(k - 2)
                 if live(k + 1):
                     h_q_of[k + 1] = quantise(h_t_of[k + 1], "h")
-                if live(k - 2):
-                    h3_q_of[k - 2] = quantise(h3_t_of[k - 2], "h3")
                 if live(k - 3):
-                    bias_store(k - 3)
+                    h3_q_of[k - 3] = quantise(h3_t_of[k - 3], "h3")
+                if live(k - 4):
+                    bias_store(k - 4)

@@ -23,7 +23,6 @@ PAIR = 2
 W = PAIR * P
 PAIRS = TILES // PAIR
 UNITS = PAIRS * CODES
-GPSIMD_TOKENS = 128
 
 FLOPS = 2 * TOKENS * CODES * HID * (HID + OUT)
 
@@ -107,7 +106,7 @@ def tile_linearwdecoder_pb_t_e_kernel(tc, h, W3_words, W3_scales, b3, Wo_words, 
 
         def copy_h_t(k):
             h_t = four.tile([P, W, PACK], BF16, align_bytes=64, name="h_t")
-            nc.vector.tensor_copy(out=h_t[:].bitcast(F32), in_=tp_of[k][:].rearrange("p u w -> p w u"))
+            nc.scalar.copy(out=h_t[:].bitcast(F32), in_=tp_of[k][:].rearrange("p u w -> p w u"))
             h_t_of[k] = h_t
 
         def quantise(values, name):
@@ -165,14 +164,7 @@ def tile_linearwdecoder_pb_t_e_kernel(tc, h, W3_words, W3_scales, b3, Wo_words, 
 
         def add_residual(k):
             h3_t = two.tile([P, W, PACK], BF16, align_bytes=64, name="h3_t")
-            r_by_token = r_of[k][:].rearrange("p t w -> p w t")
-            cut = W - GPSIMD_TOKENS
-            nc.vector.tensor_tensor(
-                out=h3_t[:, 0:cut, :], in0=r_by_token[:, 0:cut, :], in1=h_t_of[k][:, 0:cut, :], op=ADD
-            )
-            nc.gpsimd.tensor_tensor(
-                out=h3_t[:, cut:W, :], in0=r_by_token[:, cut:W, :], in1=h_t_of[k][:, cut:W, :], op=ADD
-            )
+            nc.vector.tensor_tensor(out=h3_t[:], in0=r_of[k][:].rearrange("p t w -> p w t"), in1=h_t_of[k][:], op=ADD)
             h3_t_of[k] = h3_t
 
         def second_layer(k):
@@ -205,25 +197,26 @@ def tile_linearwdecoder_pb_t_e_kernel(tc, h, W3_words, W3_scales, b3, Wo_words, 
             return 0 <= k < UNITS
 
         with tc.manual_schedule():
-            for k in range(-2, UNITS + 4):
+            for k in range(-2, UNITS + 3):
                 if live(k):
                     first_layer(k)
+                if live(k + 1):
+                    copy_h_t(k + 1)
+                if live(k):
                     copy_x(k)
-                if live(k - 4):
-                    second_layer(k - 4)
+                if live(k - 3):
+                    second_layer(k - 3)
                 if live(k + 2):
                     transpose_h(k + 2)
                 if live(k):
                     transpose_x(k)
                 if live(k - 1):
                     bias_relu(k - 1)
-                if live(k + 1):
-                    copy_h_t(k + 1)
                 if live(k - 2):
                     add_residual(k - 2)
                 if live(k + 1):
                     h_q_of[k + 1] = quantise(h_t_of[k + 1], "h")
+                if live(k - 2):
+                    h3_q_of[k - 2] = quantise(h3_t_of[k - 2], "h3")
                 if live(k - 3):
-                    h3_q_of[k - 3] = quantise(h3_t_of[k - 3], "h3")
-                if live(k - 4):
-                    bias_store(k - 4)
+                    bias_store(k - 3)

@@ -19,10 +19,12 @@ CODES = 4
 HID = 512
 OUT = 128
 TILES = TOKENS // P
-PAIR = 2
-W = PAIR * P
-PAIRS = TILES // PAIR
-UNITS = PAIRS * CODES
+QUAD = 4
+W = QUAD * P
+HALF = W // 2
+QUADS = TILES // QUAD
+UNITS = QUADS * CODES
+H_BUFS = 4
 
 FLOPS = 2 * TOKENS * CODES * HID * (HID + OUT)
 
@@ -34,53 +36,63 @@ def tile_linearwdecoder_pb_t_e_kernel(tc, h, W3_words, W3_scales, b3, Wo_words, 
 
     with ExitStack() as stack:
         keep = stack.enter_context(tc.tile_pool(name="keep", bufs=1))
-        h_pool = stack.enter_context(tc.tile_pool(name="h_pool", bufs=PAIRS))
+        h_pool = stack.enter_context(tc.tile_pool(name="h_pool", bufs=H_BUFS))
         two = stack.enter_context(tc.tile_pool(name="two", bufs=2))
+        three = stack.enter_context(tc.tile_pool(name="three", bufs=3))
         four = stack.enter_context(tc.tile_pool(name="four", bufs=4))
-        ps_one = stack.enter_context(tc.psum_pool(name="ps_one", bufs=1))
         ps_two = stack.enter_context(tc.psum_pool(name="ps_two", bufs=2))
+        ps_four = stack.enter_context(tc.psum_pool(name="ps_four", bufs=4))
 
-        h_pairs = []
-        for j in range(PAIRS):
-            h_pairs.append(h_pool.tile([P, PAIR, CODES * HID], BF16, name="h_pair"))
-        nc.sync.dma_start(out=h_pairs[0][:], in_=h_view[:, 0:PAIR, :])
+        h_quads = {}
 
-        w3_scales = keep.tile([P, CODES, HID], U8, align_bytes=64)
+        def load_h(j, by_code):
+            h_quad = h_pool.tile([P, QUAD, CODES * HID], BF16, name="h_quad")
+            tiles = slice(j * QUAD, (j + 1) * QUAD)
+            if by_code:
+                for g in range(CODES):
+                    cols = slice(g * HID, (g + 1) * HID)
+                    nc.sync.dma_start(out=h_quad[:, :, cols], in_=h_view[:, tiles, cols])
+            else:
+                nc.sync.dma_start(out=h_quad[:], in_=h_view[:, tiles, :])
+            h_quads[j] = h_quad
+
+        w3_scales_raw = keep.tile([P, CODES, HID], U8, align_bytes=64)
         wo_scales = keep.tile([P, CODES, OUT], U8, align_bytes=64)
-        nc.vector.memset(w3_scales[:].rearrange("p g n -> p (g n)").bitcast(I32), 0)
+        nc.vector.memset(w3_scales_raw[:].rearrange("p g n -> p (g n)").bitcast(I32), 0)
         nc.vector.memset(wo_scales[:].rearrange("p g n -> p (g n)").bitcast(I32), 0)
         for quad in range(4):
             rows = slice(4 * quad, 4 * quad + 4)
-            live = slice(32 * quad, 32 * quad + 4)
+            live_rows = slice(32 * quad, 32 * quad + 4)
             nc.sync.dma_start(
-                out=w3_scales[live, :, :].bitcast(I32),
+                out=w3_scales_raw[live_rows, :, :].bitcast(I32),
                 in_=W3_scales[:, rows, :].rearrange("g r n -> r g n").bitcast(I32),
             )
             nc.sync.dma_start(
-                out=wo_scales[live, :, :].bitcast(I32),
+                out=wo_scales[live_rows, :, :].bitcast(I32),
                 in_=Wo_scales[:, rows, :].rearrange("g r n -> r g n").bitcast(I32),
             )
-        w3_words = keep.tile([P, CODES, HID], U32, align_bytes=64)
-        nc.sync.dma_start(out=w3_words[:].bitcast(I32), in_=W3_words.rearrange("g p n t -> p g (n t)").bitcast(I32))
-        wo_words = keep.tile([P, CODES, OUT], U32, align_bytes=64)
-        nc.sync.dma_start(out=wo_words[:].bitcast(I32), in_=Wo_words.rearrange("g p n t -> p g (n t)").bitcast(I32))
-        for j in range(1, PAIRS):
-            nc.sync.dma_start(out=h_pairs[j][:], in_=h_view[:, j * PAIR : (j + 1) * PAIR, :])
+        load_h(0, True)
+        w3_raw = keep.tile([P, CODES, HID], I32, align_bytes=64)
+        nc.sync.dma_start(out=w3_raw[:], in_=W3_words.rearrange("g p n t -> p g (n t)").bitcast(I32))
+        wo_words = keep.tile([P, CODES, OUT], I32, align_bytes=64)
+        nc.sync.dma_start(out=wo_words[:], in_=Wo_words.rearrange("g p n t -> p g (n t)").bitcast(I32))
+        for j in range(1, H_BUFS):
+            load_h(j, False)
 
         ident = keep.tile([P, P], F32)
         make_identity(nc, ident[:])
 
         bo_row = keep.tile([P, CODES * OUT], BF16)
         nc.scalar.dma_start(out=bo_row[:], in_=bo.rearrange("g o -> (g o)").partition_broadcast(P))
-        bo_rep = keep.tile([P, PAIR, CODES * OUT], F32)
-        for s in range(PAIR):
+        bo_rep = keep.tile([P, QUAD, CODES * OUT], F32)
+        for s in range(QUAD):
             nc.vector.tensor_copy(out=bo_rep[:, s, :], in_=bo_row[:])
         b3_rows = keep.tile([P, HID], BF16)
         nc.vector.memset(b3_rows[:], 0.0)
         nc.scalar.dma_start(out=b3_rows[0:CODES, :], in_=b3)
         b3_sorted = keep.tile([P, PACK, P], F32)
         nc.vector.tensor_copy(out=b3_sorted[:], in_=b3_rows[:].rearrange("r (p t) -> r t p", t=PACK))
-        b3_t = ps_one.tile([P, PACK, P], F32, tag="o")
+        b3_t = ps_two.tile([P, PACK, P], F32, tag="o")
         for t in range(PACK):
             nc.tensor.transpose(b3_t[:, t, :], b3_sorted[:, t, :], ident[:])
         b3_cols = keep.tile([P, CODES * PACK], F32)
@@ -89,29 +101,45 @@ def tile_linearwdecoder_pb_t_e_kernel(tc, h, W3_words, W3_scales, b3, Wo_words, 
             in_=b3_t[:, :, 0:CODES].rearrange("p t g -> p g t"),
         )
 
-        tp_of, h_t_of, h_q_of, x_of, xs_of, z_of, r_of, h3_t_of, h3_q_of, o_of, o_sb_of = (
-            {}, {}, {}, {}, {}, {}, {}, {}, {}, {}, {},
-        )
+        w3_words = keep.tile([P, CODES, HID], I32, align_bytes=64)
+        w3_scales = keep.tile([P, CODES, HID], U8, align_bytes=64)
+        for g in range(CODES):
+            nc.vector.tensor_copy(
+                out=w3_scales[:, g, :].rearrange("p (t m) -> p m t", t=PACK),
+                in_=w3_scales_raw[:, g, :].rearrange("p (m t) -> p m t", t=PACK),
+            )
+            nc.vector.tensor_copy(
+                out=w3_words[:, g, :].rearrange("p (t m) -> p t m", t=PACK),
+                in_=w3_raw[:, g, :].rearrange("p (m t) -> p t m", t=PACK),
+            )
+
+        tp_of, h_t_of, h_q_of, x_of, r_of, h3_t_of, h3_q_of, o_of, o_sb_of = ({}, {}, {}, {}, {}, {}, {}, {}, {})
 
         def transpose_h(k):
             j, g = divmod(k, CODES)
-            tp = ps_one.tile([P, 2, W], F32, name="tp")
-            for s in range(PAIR):
-                words = h_pairs[j][:, s, :].bitcast(F32)
-                for u in range(2):
-                    nc.tensor.transpose(
-                        tp[:, u, s * P : (s + 1) * P], words[:, 256 * g + u : 256 * (g + 1) : 2], ident[:]
-                    )
-            tp_of[k] = tp
+            tp_of[k] = []
+            for a in range(2):
+                tp = ps_two.tile([P, 2, HALF], F32, name="tp")
+                for s in range(2):
+                    words = h_quads[j][:, 2 * a + s, :].bitcast(F32)
+                    for u in range(2):
+                        nc.tensor.transpose(
+                            tp[:, u, s * P : (s + 1) * P], words[:, 256 * g + u : 256 * (g + 1) : 2], ident[:]
+                        )
+                tp_of[k].append(tp)
 
         def copy_h_t(k):
             h_t = four.tile([P, W, PACK], BF16, align_bytes=64, name="h_t")
-            nc.scalar.copy(out=h_t[:].bitcast(F32), in_=tp_of[k][:].rearrange("p u w -> p w u"))
+            for a in range(2):
+                nc.scalar.copy(
+                    out=h_t[:, a * HALF : (a + 1) * HALF, :].bitcast(F32),
+                    in_=tp_of[k][a][:].rearrange("p u w -> p w u"),
+                )
             h_t_of[k] = h_t
 
-        def quantise(values, name):
-            codes = two.tile([P, W], U32, align_bytes=64, name=name + "_codes")
-            scales = two.tile([P, W], U8, align_bytes=64, name=name + "_scales")
+        def quantise(values, pool, name):
+            codes = pool.tile([P, W], U32, align_bytes=64, name=name + "_codes")
+            scales = pool.tile([P, W], U8, align_bytes=64, name=name + "_scales")
             nc.vector.quantize_mx(
                 out=codes[:].bitcast(FP8X4), scales=scales[:], in_=values[:].rearrange("p w t -> p (w t)")
             )
@@ -121,41 +149,27 @@ def tile_linearwdecoder_pb_t_e_kernel(tc, h, W3_words, W3_scales, b3, Wo_words, 
             g = k % CODES
             codes, scales = h_q_of[k]
             x_of[k] = []
-            for s in range(PAIR):
-                cols = slice(s * P, (s + 1) * P)
-                x = ps_two.tile([P, HID], F32, name="x")
+            for t in range(PACK):
+                cols = slice(t * P, (t + 1) * P)
+                x = ps_four.tile([P, W], F32, name="x")
                 nc.tensor.matmul_mx(
                     out=x[:],
-                    lhsT=codes[:, cols].bitcast(FP8X4),
-                    lhsT_scale=scales[:, cols],
-                    rhs=w3_words[:, g, :].bitcast(FP8X4),
-                    rhs_scale=w3_scales[:, g, :],
+                    lhsT=w3_words[:, g, cols].bitcast(FP8X4),
+                    lhsT_scale=w3_scales[:, g, cols],
+                    rhs=codes[:].bitcast(FP8X4),
+                    rhs_scale=scales[:],
                     start=True,
                     stop=True,
                 )
                 x_of[k].append(x)
 
-        def copy_x(k):
-            xs_of[k] = []
-            for s in range(PAIR):
-                x_sorted = four.tile([P, PACK, P], F32, name="x_sorted")
-                nc.scalar.copy(out=x_sorted[:], in_=x_of[k][s][:].rearrange("w (p t) -> w t p", t=PACK))
-                xs_of[k].append(x_sorted)
-
-        def transpose_x(k):
-            z = [ps_two.tile([P, 2, W], F32, name="z_lo"), ps_two.tile([P, 2, W], F32, name="z_hi")]
-            for s in range(PAIR):
-                for t in range(PACK):
-                    nc.tensor.transpose(z[t // 2][:, t % 2, s * P : (s + 1) * P], xs_of[k][s][:, t, :], ident[:])
-            z_of[k] = z
-
         def bias_relu(k):
             g = k % CODES
-            r = two.tile([P, PACK, W], F32, name="r")
+            r = three.tile([P, PACK, W], F32, name="r")
             for t in range(PACK):
                 nc.scalar.activation(
                     out=r[:, t, :],
-                    in_=z_of[k][t // 2][:, t % 2, :],
+                    in_=x_of[k][t][:],
                     func=RELU,
                     bias=b3_cols[:, PACK * g + t : PACK * g + t + 1],
                     scale=1.0,
@@ -170,8 +184,8 @@ def tile_linearwdecoder_pb_t_e_kernel(tc, h, W3_words, W3_scales, b3, Wo_words, 
         def second_layer(k):
             g = k % CODES
             codes, scales = h3_q_of[k]
-            o = ps_one.tile([P, PAIR, OUT], F32, name="o")
-            for s in range(PAIR):
+            o = ps_two.tile([P, QUAD, OUT], F32, name="o")
+            for s in range(QUAD):
                 cols = slice(s * P, (s + 1) * P)
                 nc.tensor.matmul_mx(
                     out=o[:, s, :],
@@ -187,11 +201,11 @@ def tile_linearwdecoder_pb_t_e_kernel(tc, h, W3_words, W3_scales, b3, Wo_words, 
         def bias_store(k):
             j, g = divmod(k, CODES)
             if g == 0:
-                o_sb_of[j] = two.tile([P, PAIR, CODES * OUT], F32, name="o_sb")
+                o_sb_of[j] = two.tile([P, QUAD, CODES * OUT], F32, name="o_sb")
             cols = slice(g * OUT, (g + 1) * OUT)
             nc.vector.tensor_tensor(out=o_sb_of[j][:, :, cols], in0=o_of[k][:], in1=bo_rep[:, :, cols], op=ADD)
             if g == CODES - 1:
-                nc.sync.dma_start(out=out_view[:, j * PAIR : (j + 1) * PAIR, :], in_=o_sb_of[j][:])
+                nc.sync.dma_start(out=out_view[:, j * QUAD : (j + 1) * QUAD, :], in_=o_sb_of[j][:])
 
         def live(k):
             return 0 <= k < UNITS
@@ -200,23 +214,20 @@ def tile_linearwdecoder_pb_t_e_kernel(tc, h, W3_words, W3_scales, b3, Wo_words, 
             for k in range(-2, UNITS + 3):
                 if live(k):
                     first_layer(k)
-                if live(k + 1):
-                    copy_h_t(k + 1)
-                if live(k):
-                    copy_x(k)
-                if live(k - 3):
-                    second_layer(k - 3)
+                    bias_relu(k)
                 if live(k + 2):
                     transpose_h(k + 2)
-                if live(k):
-                    transpose_x(k)
+                    copy_h_t(k + 2)
+                    j, g = divmod(k + 2, CODES)
+                    if g == CODES - 1 and j + H_BUFS < QUADS:
+                        load_h(j + H_BUFS, False)
+                if live(k - 2):
+                    second_layer(k - 2)
                 if live(k - 1):
-                    bias_relu(k - 1)
-                if live(k - 2):
-                    add_residual(k - 2)
+                    add_residual(k - 1)
                 if live(k + 1):
-                    h_q_of[k + 1] = quantise(h_t_of[k + 1], "h")
-                if live(k - 2):
-                    h3_q_of[k - 2] = quantise(h3_t_of[k - 2], "h3")
+                    h_q_of[k + 1] = quantise(h_t_of[k + 1], three, "h")
                 if live(k - 3):
                     bias_store(k - 3)
+                if live(k - 1):
+                    h3_q_of[k - 1] = quantise(h3_t_of[k - 1], two, "h3")

@@ -178,7 +178,12 @@ def tile_linearwdecoder_pb_t_e_kernel(tc, h, W3_words, W3_scales, b3, Wo_words, 
 
         def add_residual(k):
             h3_t = two.tile([P, W, PACK], BF16, align_bytes=64, name="h3_t")
-            nc.vector.tensor_tensor(out=h3_t[:], in0=r_of[k][:].rearrange("p t w -> p w t"), in1=h_t_of[k][:], op=ADD)
+            nc.vector.tensor_tensor(
+                out=h3_t[:].rearrange("p (c i) t -> p c t i", i=4),
+                in0=r_of[k][:].rearrange("p t (c i) -> p c t i", i=4),
+                in1=h_t_of[k][:].rearrange("p (c i) t -> p c t i", i=4),
+                op=ADD,
+            )
             h3_t_of[k] = h3_t
 
         def second_layer(k):

@@ -25,6 +25,7 @@ HALF = W // 2
 QUADS = TILES // QUAD
 UNITS = QUADS * CODES
 H_BUFS = 4
+G_TOKENS = 128
 
 FLOPS = 2 * TOKENS * CODES * HID * (HID + OUT)
 
@@ -40,8 +41,9 @@ def tile_linearwdecoder_pb_t_e_kernel(tc, h, W3_words, W3_scales, b3, Wo_words, 
         two = stack.enter_context(tc.tile_pool(name="two", bufs=2))
         three = stack.enter_context(tc.tile_pool(name="three", bufs=3))
         four = stack.enter_context(tc.tile_pool(name="four", bufs=4))
-        ps_two = stack.enter_context(tc.psum_pool(name="ps_two", bufs=2))
-        ps_four = stack.enter_context(tc.psum_pool(name="ps_four", bufs=4))
+        one = stack.enter_context(tc.tile_pool(name="one", bufs=1))
+        ps_one = stack.enter_context(tc.psum_pool(name="ps_one", bufs=1))
+        ps_three = stack.enter_context(tc.psum_pool(name="ps_three", bufs=3))
 
         h_quads = {}
 
@@ -92,7 +94,7 @@ def tile_linearwdecoder_pb_t_e_kernel(tc, h, W3_words, W3_scales, b3, Wo_words, 
         nc.scalar.dma_start(out=b3_rows[0:CODES, :], in_=b3)
         b3_sorted = keep.tile([P, PACK, P], F32)
         nc.vector.tensor_copy(out=b3_sorted[:], in_=b3_rows[:].rearrange("r (p t) -> r t p", t=PACK))
-        b3_t = ps_two.tile([P, PACK, P], F32, tag="o")
+        b3_t = ps_one.tile([P, PACK, P], F32, tag="o")
         for t in range(PACK):
             nc.tensor.transpose(b3_t[:, t, :], b3_sorted[:, t, :], ident[:])
         b3_cols = keep.tile([P, CODES * PACK], F32)
@@ -117,24 +119,22 @@ def tile_linearwdecoder_pb_t_e_kernel(tc, h, W3_words, W3_scales, b3, Wo_words, 
 
         def transpose_h(k):
             j, g = divmod(k, CODES)
-            tp_of[k] = []
-            for a in range(2):
-                tp = ps_two.tile([P, 2, HALF], F32, name="tp")
-                for s in range(2):
-                    words = h_quads[j][:, 2 * a + s, :].bitcast(F32)
-                    for u in range(2):
-                        nc.tensor.transpose(
-                            tp[:, u, s * P : (s + 1) * P], words[:, 256 * g + u : 256 * (g + 1) : 2], ident[:]
-                        )
-                tp_of[k].append(tp)
+            tp_kept = ps_three.tile([P, HALF, 2], F32, name="tp_kept")
+            tp_brief = ps_one.tile([P, 2, HALF], F32, name="tp_brief")
+            for s in range(QUAD):
+                words = h_quads[j][:, s, :].bitcast(F32)
+                for u in range(2):
+                    if s < 2:
+                        dest = tp_kept[:, s * P : (s + 1) * P, u]
+                    else:
+                        dest = tp_brief[:, u, (s - 2) * P : (s - 1) * P]
+                    nc.tensor.transpose(dest, words[:, 256 * g + u : 256 * (g + 1) : 2], ident[:])
+            tp_of[k] = [tp_kept, tp_brief]
 
         def copy_h_t(k):
             h_t = four.tile([P, W, PACK], BF16, align_bytes=64, name="h_t")
-            for a in range(2):
-                nc.scalar.copy(
-                    out=h_t[:, a * HALF : (a + 1) * HALF, :].bitcast(F32),
-                    in_=tp_of[k][a][:].rearrange("p u w -> p w u"),
-                )
+            nc.scalar.copy(out=h_t[:, 0:HALF, :].bitcast(F32), in_=tp_of[k][0][:])
+            nc.scalar.copy(out=h_t[:, HALF:W, :].bitcast(F32), in_=tp_of[k][1][:].rearrange("p u w -> p w u"))
             h_t_of[k] = h_t
 
         def quantise(values, pool, name):
@@ -145,13 +145,13 @@ def tile_linearwdecoder_pb_t_e_kernel(tc, h, W3_words, W3_scales, b3, Wo_words, 
             )
             return codes, scales
 
-        def first_layer(k):
+        def first_layer(k, ts):
             g = k % CODES
             codes, scales = h_q_of[k]
-            x_of[k] = []
-            for t in range(PACK):
+            x_of.setdefault(k, [])
+            for t in ts:
                 cols = slice(t * P, (t + 1) * P)
-                x = ps_four.tile([P, W], F32, name="x")
+                x = ps_three.tile([P, W], F32, name="x")
                 nc.tensor.matmul_mx(
                     out=x[:],
                     lhsT=w3_words[:, g, cols].bitcast(FP8X4),
@@ -163,10 +163,12 @@ def tile_linearwdecoder_pb_t_e_kernel(tc, h, W3_words, W3_scales, b3, Wo_words, 
                 )
                 x_of[k].append(x)
 
-        def bias_relu(k):
+        def bias_relu(k, ts):
             g = k % CODES
-            r = three.tile([P, PACK, W], F32, name="r")
-            for t in range(PACK):
+            if k not in r_of:
+                r_of[k] = three.tile([P, PACK, W], F32, name="r")
+            r = r_of[k]
+            for t in ts:
                 nc.scalar.activation(
                     out=r[:, t, :],
                     in_=x_of[k][t][:],
@@ -174,22 +176,30 @@ def tile_linearwdecoder_pb_t_e_kernel(tc, h, W3_words, W3_scales, b3, Wo_words, 
                     bias=b3_cols[:, PACK * g + t : PACK * g + t + 1],
                     scale=1.0,
                 )
-            r_of[k] = r
 
-        def add_residual(k):
-            h3_t = two.tile([P, W, PACK], BF16, align_bytes=64, name="h3_t")
+        def add_from_psum(k):
+            h3_t = one.tile([P, W, PACK], BF16, align_bytes=64, name="h3_t")
             nc.vector.tensor_tensor(
-                out=h3_t[:].rearrange("p (c i) t -> p c t i", i=4),
-                in0=r_of[k][:].rearrange("p t (c i) -> p c t i", i=4),
-                in1=h_t_of[k][:].rearrange("p (c i) t -> p c t i", i=4),
+                out=h3_t[:, 0:HALF, :].rearrange("p (c i) t -> p c t i", i=4),
+                in0=tp_of[k][0][:].bitcast(BF16).rearrange("p (c i) t -> p c t i", i=4),
+                in1=r_of[k][:, :, 0:HALF].rearrange("p t (c i) -> p c t i", i=4),
                 op=ADD,
             )
             h3_t_of[k] = h3_t
 
+        def add_from_sbuf(engine, k, first, last):
+            tokens = slice(first, last)
+            engine.tensor_tensor(
+                out=h3_t_of[k][:, tokens, :].rearrange("p (c i) t -> p c t i", i=4),
+                in0=r_of[k][:, :, tokens].rearrange("p t (c i) -> p c t i", i=4),
+                in1=h_t_of[k][:, tokens, :].rearrange("p (c i) t -> p c t i", i=4),
+                op=ADD,
+            )
+
         def second_layer(k):
             g = k % CODES
             codes, scales = h3_q_of[k]
-            o = ps_two.tile([P, QUAD, OUT], F32, name="o")
+            o = ps_one.tile([P, QUAD, OUT], F32, name="o")
             for s in range(QUAD):
                 cols = slice(s * P, (s + 1) * P)
                 nc.tensor.matmul_mx(
@@ -217,22 +227,27 @@ def tile_linearwdecoder_pb_t_e_kernel(tc, h, W3_words, W3_scales, b3, Wo_words, 
 
         with tc.manual_schedule():
             for k in range(-2, UNITS + 3):
+                if live(k - 2):
+                    second_layer(k - 2)
                 if live(k):
-                    first_layer(k)
-                    bias_relu(k)
+                    bias_relu(k, [0])
+                    first_layer(k, [3])
+                    bias_relu(k, [1, 2, 3])
                 if live(k + 2):
                     transpose_h(k + 2)
                     copy_h_t(k + 2)
                     j, g = divmod(k + 2, CODES)
                     if g == CODES - 1 and j + H_BUFS < QUADS:
                         load_h(j + H_BUFS, False)
-                if live(k - 2):
-                    second_layer(k - 2)
-                if live(k - 1):
-                    add_residual(k - 1)
                 if live(k + 1):
                     h_q_of[k + 1] = quantise(h_t_of[k + 1], three, "h")
-                if live(k - 3):
-                    bias_store(k - 3)
+                    first_layer(k + 1, [0, 1, 2])
                 if live(k - 1):
                     h3_q_of[k - 1] = quantise(h3_t_of[k - 1], two, "h3")
+                if live(k):
+                    add_from_psum(k)
+                    add_from_sbuf(nc.gpsimd, k, HALF, HALF + G_TOKENS)
+                if live(k - 2):
+                    bias_store(k - 2)
+                if live(k):
+                    add_from_sbuf(nc.vector, k, HALF + G_TOKENS, W)

@@ -244,10 +244,9 @@ def tile_linearwdecoder_pb_t_e_kernel(tc, h, W3_words, W3_scales, b3, Wo_words, 
                     first_layer(k + 1, [0, 1, 2])
                 if live(k - 1):
                     h3_q_of[k - 1] = quantise(h3_t_of[k - 1], two, "h3")
-                if live(k):
-                    add_from_psum(k)
-                    add_from_sbuf(nc.gpsimd, k, HALF, HALF + G_TOKENS)
                 if live(k - 2):
                     bias_store(k - 2)
                 if live(k):
+                    add_from_psum(k)
+                    add_from_sbuf(nc.gpsimd, k, HALF, HALF + G_TOKENS)
                     add_from_sbuf(nc.vector, k, HALF + G_TOKENS, W)

@@ -24,7 +24,7 @@ W = QUAD * P
 HALF = W // 2
 QUADS = TILES // QUAD
 UNITS = QUADS * CODES
-H_BUFS = 4
+H_BUFS = 12
 G_TOKENS = 128
 
 FLOPS = 2 * TOKENS * CODES * HID * (HID + OUT)
@@ -45,67 +45,51 @@ def tile_linearwdecoder_pb_t_e_kernel(tc, h, W3_words, W3_scales, b3, Wo_words, 
         ps_one = stack.enter_context(tc.psum_pool(name="ps_one", bufs=1))
         ps_three = stack.enter_context(tc.psum_pool(name="ps_three", bufs=3))
 
-        h_quads = {}
+        h_of = {}
 
-        def load_h(j, by_code):
-            h_quad = h_pool.tile([P, QUAD, CODES * HID], BF16, name="h_quad")
-            tiles = slice(j * QUAD, (j + 1) * QUAD)
-            if by_code:
-                for g in range(CODES):
-                    cols = slice(g * HID, (g + 1) * HID)
-                    nc.sync.dma_start(out=h_quad[:, :, cols], in_=h_view[:, tiles, cols])
-            else:
-                nc.sync.dma_start(out=h_quad[:], in_=h_view[:, tiles, :])
-            h_quads[j] = h_quad
+        def load_h(k):
+            j, g = divmod(k, CODES)
+            h_unit = h_pool.tile([P, QUAD, HID], BF16, name="h_unit")
+            nc.sync.dma_start(out=h_unit[:], in_=h_view[:, j * QUAD : (j + 1) * QUAD, g * HID : (g + 1) * HID])
+            h_of[k] = h_unit
 
+        w3_raw = keep.tile([P, CODES, HID], I32, align_bytes=64)
         w3_scales_raw = keep.tile([P, CODES, HID], U8, align_bytes=64)
         wo_scales = keep.tile([P, CODES, OUT], U8, align_bytes=64)
         nc.vector.memset(w3_scales_raw[:].rearrange("p g n -> p (g n)").bitcast(I32), 0)
         nc.vector.memset(wo_scales[:].rearrange("p g n -> p (g n)").bitcast(I32), 0)
-        for quad in range(4):
-            rows = slice(4 * quad, 4 * quad + 4)
-            live_rows = slice(32 * quad, 32 * quad + 4)
-            nc.sync.dma_start(
-                out=w3_scales_raw[live_rows, :, :].bitcast(I32),
-                in_=W3_scales[:, rows, :].rearrange("g r n -> r g n").bitcast(I32),
-            )
-            nc.sync.dma_start(
-                out=wo_scales[live_rows, :, :].bitcast(I32),
-                in_=Wo_scales[:, rows, :].rearrange("g r n -> r g n").bitcast(I32),
-            )
-        load_h(0, True)
-        w3_raw = keep.tile([P, CODES, HID], I32, align_bytes=64)
-        nc.sync.dma_start(out=w3_raw[:], in_=W3_words.rearrange("g p n t -> p g (n t)").bitcast(I32))
+
+        def load_scales(tile, scales):
+            for quad in range(4):
+                nc.sync.dma_start(
+                    out=tile[32 * quad : 32 * quad + 4, :, :].bitcast(I32),
+                    in_=scales[:, 4 * quad : 4 * quad + 4, :].rearrange("g r n -> r g n").bitcast(I32),
+                )
+
+        load_scales(w3_scales_raw, W3_scales)
+        for g in range(CODES):
+            load_h(g)
+            nc.sync.dma_start(out=w3_raw[:, g, :], in_=W3_words[g].rearrange("p n t -> p (n t)").bitcast(I32))
+        load_scales(wo_scales, Wo_scales)
         wo_words = keep.tile([P, CODES, OUT], I32, align_bytes=64)
         nc.sync.dma_start(out=wo_words[:], in_=Wo_words.rearrange("g p n t -> p g (n t)").bitcast(I32))
-        for j in range(1, H_BUFS):
-            load_h(j, False)
+        for k in range(CODES, H_BUFS):
+            load_h(k)
 
         ident = keep.tile([P, P], F32)
         make_identity(nc, ident[:])
 
+        b3_cols = keep.tile([P, CODES, PACK], BF16)
+        nc.scalar.dma_start(out=b3_cols[:], in_=b3.rearrange("g (p t) -> p g t", t=PACK))
         bo_row = keep.tile([P, CODES * OUT], BF16)
         nc.scalar.dma_start(out=bo_row[:], in_=bo.rearrange("g o -> (g o)").partition_broadcast(P))
         bo_rep = keep.tile([P, QUAD, CODES * OUT], F32)
         for s in range(QUAD):
-            nc.vector.tensor_copy(out=bo_rep[:, s, :], in_=bo_row[:])
-        b3_rows = keep.tile([P, HID], BF16)
-        nc.vector.memset(b3_rows[:], 0.0)
-        nc.scalar.dma_start(out=b3_rows[0:CODES, :], in_=b3)
-        b3_sorted = keep.tile([P, PACK, P], F32)
-        nc.vector.tensor_copy(out=b3_sorted[:], in_=b3_rows[:].rearrange("r (p t) -> r t p", t=PACK))
-        b3_t = ps_one.tile([P, PACK, P], F32, tag="o")
-        for t in range(PACK):
-            nc.tensor.transpose(b3_t[:, t, :], b3_sorted[:, t, :], ident[:])
-        b3_cols = keep.tile([P, CODES * PACK], F32)
-        nc.vector.tensor_copy(
-            out=b3_cols[:].rearrange("p (g t) -> p g t", t=PACK),
-            in_=b3_t[:, :, 0:CODES].rearrange("p t g -> p g t"),
-        )
-
+            nc.gpsimd.tensor_copy(out=bo_rep[:, s, :], in_=bo_row[:])
         w3_words = keep.tile([P, CODES, HID], I32, align_bytes=64)
         w3_scales = keep.tile([P, CODES, HID], U8, align_bytes=64)
-        for g in range(CODES):
+
+        def sort_w3(g):
             nc.vector.tensor_copy(
                 out=w3_scales[:, g, :].rearrange("p (t m) -> p m t", t=PACK),
                 in_=w3_scales_raw[:, g, :].rearrange("p (m t) -> p m t", t=PACK),
@@ -118,17 +102,16 @@ def tile_linearwdecoder_pb_t_e_kernel(tc, h, W3_words, W3_scales, b3, Wo_words, 
         tp_of, h_t_of, h_q_of, x_of, r_of, h3_t_of, h3_q_of, o_of, o_sb_of = ({}, {}, {}, {}, {}, {}, {}, {}, {})
 
         def transpose_h(k):
-            j, g = divmod(k, CODES)
             tp_kept = ps_three.tile([P, HALF, 2], F32, name="tp_kept")
             tp_brief = ps_one.tile([P, 2, HALF], F32, name="tp_brief")
             for s in range(QUAD):
-                words = h_quads[j][:, s, :].bitcast(F32)
+                words = h_of[k][:, s, :].bitcast(F32)
                 for u in range(2):
                     if s < 2:
                         dest = tp_kept[:, s * P : (s + 1) * P, u]
                     else:
                         dest = tp_brief[:, u, (s - 2) * P : (s - 1) * P]
-                    nc.tensor.transpose(dest, words[:, 256 * g + u : 256 * (g + 1) : 2], ident[:])
+                    nc.tensor.transpose(dest, words[:, u : HID // 2 : 2], ident[:])
             tp_of[k] = [tp_kept, tp_brief]
 
         def copy_h_t(k):
@@ -173,7 +156,7 @@ def tile_linearwdecoder_pb_t_e_kernel(tc, h, W3_words, W3_scales, b3, Wo_words, 
                     out=r[:, t, :],
                     in_=x_of[k][t][:],
                     func=RELU,
-                    bias=b3_cols[:, PACK * g + t : PACK * g + t + 1],
+                    bias=b3_cols[:, g, t : t + 1],
                     scale=1.0,
                 )
 
@@ -219,8 +202,11 @@ def tile_linearwdecoder_pb_t_e_kernel(tc, h, W3_words, W3_scales, b3, Wo_words, 
                 o_sb_of[j] = two.tile([P, QUAD, CODES * OUT], F32, name="o_sb")
             cols = slice(g * OUT, (g + 1) * OUT)
             nc.vector.tensor_tensor(out=o_sb_of[j][:, :, cols], in0=o_of[k][:], in1=bo_rep[:, :, cols], op=ADD)
-            if g == CODES - 1:
-                nc.sync.dma_start(out=out_view[:, j * QUAD : (j + 1) * QUAD, :], in_=o_sb_of[j][:])
+            tiles = slice(j * QUAD, (j + 1) * QUAD)
+            if j == QUADS - 1:
+                nc.sync.dma_start(out=out_view[:, tiles, cols], in_=o_sb_of[j][:, :, cols])
+            elif g == CODES - 1:
+                nc.sync.dma_start(out=out_view[:, tiles, :], in_=o_sb_of[j][:])
 
         def live(k):
             return 0 <= k < UNITS
@@ -236,12 +222,15 @@ def tile_linearwdecoder_pb_t_e_kernel(tc, h, W3_words, W3_scales, b3, Wo_words, 
                 if live(k + 2):
                     transpose_h(k + 2)
                     copy_h_t(k + 2)
-                    j, g = divmod(k + 2, CODES)
-                    if g == CODES - 1 and j + H_BUFS < QUADS:
-                        load_h(j + H_BUFS, False)
+                    if live(k + 2 + H_BUFS):
+                        load_h(k + 2 + H_BUFS)
+                if k + 2 == 0:
+                    sort_w3(0)
                 if live(k + 1):
                     h_q_of[k + 1] = quantise(h_t_of[k + 1], three, "h")
                     first_layer(k + 1, [0, 1, 2])
+                if 0 < k + 2 < CODES:
+                    sort_w3(k + 2)
                 if live(k - 1):
                     h3_q_of[k - 1] = quantise(h3_t_of[k - 1], two, "h3")
                 if live(k - 2):

@@ -25,7 +25,7 @@ HALF = W // 2
 QUADS = TILES // QUAD
 UNITS = QUADS * CODES
 H_BUFS = 12
-G_TOKENS = 128
+G_TOKENS = 168
 
 FLOPS = 2 * TOKENS * CODES * HID * (HID + OUT)
 
@@ -128,6 +128,18 @@ def tile_linearwdecoder_pb_t_e_kernel(tc, h, W3_words, W3_scales, b3, Wo_words, 
             )
             return codes, scales
 
+        def quantise_h3(k):
+            codes = two.tile([P, W], U32, align_bytes=64, name="h3_codes")
+            scales = two.tile([P, W], U8, align_bytes=64, name="h3_scales")
+            for a in (1, 0):
+                cols = slice(a * HALF, (a + 1) * HALF)
+                nc.vector.quantize_mx(
+                    out=codes[:, cols].bitcast(FP8X4),
+                    scales=scales[:, cols],
+                    in_=h3_t_of[k][a][:].rearrange("p w t -> p (w t)"),
+                )
+            return codes, scales
+
         def first_layer(k, ts):
             g = k % CODES
             codes, scales = h_q_of[k]
@@ -161,19 +173,20 @@ def tile_linearwdecoder_pb_t_e_kernel(tc, h, W3_words, W3_scales, b3, Wo_words, 
                 )
 
         def add_from_psum(k):
-            h3_t = one.tile([P, W, PACK], BF16, align_bytes=64, name="h3_t")
+            h3_front = one.tile([P, HALF, PACK], BF16, align_bytes=64, name="h3_front")
+            h3_back = one.tile([P, HALF, PACK], BF16, align_bytes=64, name="h3_back")
             nc.vector.tensor_tensor(
-                out=h3_t[:, 0:HALF, :].rearrange("p (c i) t -> p c t i", i=4),
+                out=h3_front[:].rearrange("p (c i) t -> p c t i", i=4),
                 in0=tp_of[k][0][:].bitcast(BF16).rearrange("p (c i) t -> p c t i", i=4),
                 in1=r_of[k][:, :, 0:HALF].rearrange("p t (c i) -> p c t i", i=4),
                 op=ADD,
             )
-            h3_t_of[k] = h3_t
+            h3_t_of[k] = [h3_front, h3_back]
 
         def add_from_sbuf(engine, k, first, last):
             tokens = slice(first, last)
             engine.tensor_tensor(
-                out=h3_t_of[k][:, tokens, :].rearrange("p (c i) t -> p c t i", i=4),
+                out=h3_t_of[k][1][:, first - HALF : last - HALF, :].rearrange("p (c i) t -> p c t i", i=4),
                 in0=r_of[k][:, :, tokens].rearrange("p t (c i) -> p c t i", i=4),
                 in1=h_t_of[k][:, tokens, :].rearrange("p (c i) t -> p c t i", i=4),
                 op=ADD,
@@ -232,7 +245,7 @@ def tile_linearwdecoder_pb_t_e_kernel(tc, h, W3_words, W3_scales, b3, Wo_words, 
                 if 0 < k + 2 < CODES:
                     sort_w3(k + 2)
                 if live(k - 1):
-                    h3_q_of[k - 1] = quantise(h3_t_of[k - 1], two, "h3")
+                    h3_q_of[k - 1] = quantise_h3(k - 1)
                 if live(k - 2):
                     bias_store(k - 2)
                 if live(k):

@@ -73,6 +73,8 @@ def tile_linearwdecoder_pb_t_e_kernel(tc, h, W3_words, W3_scales, b3, Wo_words, 
         load_scales(wo_scales, Wo_scales)
         wo_words = keep.tile([P, CODES, OUT], I32, align_bytes=64)
         nc.sync.dma_start(out=wo_words[:], in_=Wo_words.rearrange("g p n t -> p g (n t)").bitcast(I32))
+        bo_row = keep.tile([P, CODES * OUT], BF16)
+        nc.sync.dma_start(out=bo_row[:], in_=bo.rearrange("g o -> (g o)").partition_broadcast(P))
         for k in range(CODES, H_BUFS):
             load_h(k)
 
@@ -81,11 +83,6 @@ def tile_linearwdecoder_pb_t_e_kernel(tc, h, W3_words, W3_scales, b3, Wo_words, 
 
         b3_cols = keep.tile([P, CODES, PACK], BF16)
         nc.scalar.dma_start(out=b3_cols[:], in_=b3.rearrange("g (p t) -> p g t", t=PACK))
-        bo_row = keep.tile([P, CODES * OUT], BF16)
-        nc.scalar.dma_start(out=bo_row[:], in_=bo.rearrange("g o -> (g o)").partition_broadcast(P))
-        bo_rep = keep.tile([P, QUAD, CODES * OUT], F32)
-        for s in range(QUAD):
-            nc.gpsimd.tensor_copy(out=bo_rep[:, s, :], in_=bo_row[:])
         w3_words = keep.tile([P, CODES, HID], I32, align_bytes=64)
         w3_scales = keep.tile([P, CODES, HID], U8, align_bytes=64)
 
@@ -214,7 +211,12 @@ def tile_linearwdecoder_pb_t_e_kernel(tc, h, W3_words, W3_scales, b3, Wo_words, 
             if g == 0:
                 o_sb_of[j] = two.tile([P, QUAD, CODES * OUT], F32, name="o_sb")
             cols = slice(g * OUT, (g + 1) * OUT)
-            nc.vector.tensor_tensor(out=o_sb_of[j][:, :, cols], in0=o_of[k][:], in1=bo_rep[:, :, cols], op=ADD)
+            nc.vector.tensor_tensor(
+                out=o_sb_of[j][:, :, cols],
+                in0=o_of[k][:],
+                in1=bo_row[:, cols].unsqueeze(1).to_broadcast([P, QUAD, OUT]),
+                op=ADD,
+            )
             tiles = slice(j * QUAD, (j + 1) * QUAD)
             if j == QUADS - 1:
                 nc.sync.dma_start(out=out_view[:, tiles, cols], in_=o_sb_of[j][:, :, cols])

@@ -26,6 +26,8 @@ QUADS = TILES // QUAD
 UNITS = QUADS * CODES
 H_BUFS = 12
 G_TOKENS = 168
+LAST = UNITS - 1
+G_TOKENS_LAST = 96
 
 FLOPS = 2 * TOKENS * CODES * HID * (HID + OUT)
 
@@ -67,9 +69,17 @@ def tile_linearwdecoder_pb_t_e_kernel(tc, h, W3_words, W3_scales, b3, Wo_words, 
                 )
 
         load_scales(w3_scales_raw, W3_scales)
-        for g in range(CODES):
-            load_h(g)
+        def load_w3(g):
             nc.sync.dma_start(out=w3_raw[:, g, :], in_=W3_words[g].rearrange("p n t -> p (n t)").bitcast(I32))
+
+        load_h(0)
+        load_w3(0)
+        load_h(1)
+        load_w3(1)
+        load_w3(2)
+        load_w3(3)
+        load_h(2)
+        load_h(3)
         load_scales(wo_scales, Wo_scales)
         wo_words = keep.tile([P, CODES, OUT], I32, align_bytes=64)
         nc.sync.dma_start(out=wo_words[:], in_=Wo_words.rearrange("g p n t -> p g (n t)").bitcast(I32))
@@ -97,6 +107,7 @@ def tile_linearwdecoder_pb_t_e_kernel(tc, h, W3_words, W3_scales, b3, Wo_words, 
             )
 
         tp_of, h_t_of, h_q_of, x_of, r_of, h3_t_of, h3_q_of, o_of, o_sb_of = ({}, {}, {}, {}, {}, {}, {}, {}, {})
+        r_whole_of = {}
 
         def transpose_h(k):
             tp_kept = ps_three.tile([P, HALF, 2], F32, name="tp_kept")
@@ -125,17 +136,22 @@ def tile_linearwdecoder_pb_t_e_kernel(tc, h, W3_words, W3_scales, b3, Wo_words, 
             )
             return codes, scales
 
+        def quantise_h3_half(k, a):
+            if k not in h3_q_of:
+                codes = two.tile([P, W], U32, align_bytes=64, name="h3_codes")
+                scales = two.tile([P, W], U8, align_bytes=64, name="h3_scales")
+                h3_q_of[k] = (codes, scales)
+            codes, scales = h3_q_of[k]
+            cols = slice(a * HALF, (a + 1) * HALF)
+            nc.vector.quantize_mx(
+                out=codes[:, cols].bitcast(FP8X4),
+                scales=scales[:, cols],
+                in_=h3_t_of[k][a][:].rearrange("p w t -> p (w t)"),
+            )
+
         def quantise_h3(k):
-            codes = two.tile([P, W], U32, align_bytes=64, name="h3_codes")
-            scales = two.tile([P, W], U8, align_bytes=64, name="h3_scales")
-            for a in (1, 0):
-                cols = slice(a * HALF, (a + 1) * HALF)
-                nc.vector.quantize_mx(
-                    out=codes[:, cols].bitcast(FP8X4),
-                    scales=scales[:, cols],
-                    in_=h3_t_of[k][a][:].rearrange("p w t -> p (w t)"),
-                )
-            return codes, scales
+            quantise_h3_half(k, 1)
+            quantise_h3_half(k, 0)
 
         def first_layer(k, ts):
             g = k % CODES
@@ -143,7 +159,7 @@ def tile_linearwdecoder_pb_t_e_kernel(tc, h, W3_words, W3_scales, b3, Wo_words, 
             x_of.setdefault(k, [])
             for t in ts:
                 cols = slice(t * P, (t + 1) * P)
-                x = ps_three.tile([P, W], F32, name="x")
+                x = ps_three.tile([P, W], F32, name="tp_kept" if (k == LAST and t == 3) else "x")
                 nc.tensor.matmul_mx(
                     out=x[:],
                     lhsT=w3_words[:, g, cols].bitcast(FP8X4),
@@ -157,9 +173,10 @@ def tile_linearwdecoder_pb_t_e_kernel(tc, h, W3_words, W3_scales, b3, Wo_words, 
 
         def bias_relu(k, ts):
             g = k % CODES
-            if k not in r_of:
-                r_of[k] = three.tile([P, PACK, W], F32, name="r")
-            r = r_of[k]
+            if k not in r_whole_of:
+                r_whole_of[k] = three.tile([P, PACK, W], F32, name="r")
+                r_of[k] = [r_whole_of[k][:, :, 0:HALF], r_whole_of[k][:, :, HALF:W]]
+            r = r_whole_of[k]
             for t in ts:
                 nc.scalar.activation(
                     out=r[:, t, :],
@@ -169,13 +186,26 @@ def tile_linearwdecoder_pb_t_e_kernel(tc, h, W3_words, W3_scales, b3, Wo_words, 
                     scale=1.0,
                 )
 
+        def bias_relu_half(k, a):
+            g = k % CODES
+            r_half = one.tile([P, PACK, HALF], F32, name="r_half%d" % a)
+            for t in range(PACK):
+                nc.scalar.activation(
+                    out=r_half[:, t, :],
+                    in_=x_of[k][t][:, a * HALF : (a + 1) * HALF],
+                    func=RELU,
+                    bias=b3_cols[:, g, t : t + 1],
+                    scale=1.0,
+                )
+            r_of.setdefault(k, []).append(r_half[:])
+
         def add_from_psum(k):
             h3_front = one.tile([P, HALF, PACK], BF16, align_bytes=64, name="h3_front")
             h3_back = one.tile([P, HALF, PACK], BF16, align_bytes=64, name="h3_back")
             nc.vector.tensor_tensor(
                 out=h3_front[:].rearrange("p (c i) t -> p c t i", i=4),
                 in0=tp_of[k][0][:].bitcast(BF16).rearrange("p (c i) t -> p c t i", i=4),
-                in1=r_of[k][:, :, 0:HALF].rearrange("p t (c i) -> p c t i", i=4),
+                in1=r_of[k][0].rearrange("p t (c i) -> p c t i", i=4),
                 op=ADD,
             )
             h3_t_of[k] = [h3_front, h3_back]
@@ -184,16 +214,16 @@ def tile_linearwdecoder_pb_t_e_kernel(tc, h, W3_words, W3_scales, b3, Wo_words, 
             tokens = slice(first, last)
             engine.tensor_tensor(
                 out=h3_t_of[k][1][:, first - HALF : last - HALF, :].rearrange("p (c i) t -> p c t i", i=4),
-                in0=r_of[k][:, :, tokens].rearrange("p t (c i) -> p c t i", i=4),
+                in0=r_of[k][1][:, :, first - HALF : last - HALF].rearrange("p t (c i) -> p c t i", i=4),
                 in1=h_t_of[k][:, tokens, :].rearrange("p (c i) t -> p c t i", i=4),
                 op=ADD,
             )
 
-        def second_layer(k):
+        def second_layer(k, first=0, n=QUAD, bank="o"):
             g = k % CODES
             codes, scales = h3_q_of[k]
-            o = ps_one.tile([P, QUAD, OUT], F32, name="o")
-            for s in range(QUAD):
+            o = ps_one.tile([P, QUAD, OUT], F32, name=bank)
+            for s in range(first, first + n):
                 cols = slice(s * P, (s + 1) * P)
                 nc.tensor.matmul_mx(
                     out=o[:, s, :],
@@ -206,28 +236,28 @@ def tile_linearwdecoder_pb_t_e_kernel(tc, h, W3_words, W3_scales, b3, Wo_words, 
                 )
             o_of[k] = o
 
-        def bias_store(k):
+        def bias_store(k, first=0, n=QUAD):
             j, g = divmod(k, CODES)
-            if g == 0:
+            if j not in o_sb_of:
                 o_sb_of[j] = two.tile([P, QUAD, CODES * OUT], F32, name="o_sb")
             cols = slice(g * OUT, (g + 1) * OUT)
+            rows = slice(first, first + n)
             nc.vector.tensor_tensor(
-                out=o_sb_of[j][:, :, cols],
-                in0=o_of[k][:],
-                in1=bo_row[:, cols].unsqueeze(1).to_broadcast([P, QUAD, OUT]),
+                out=o_sb_of[j][:, rows, cols],
+                in0=o_of[k][:, rows, :],
+                in1=bo_row[:, cols].unsqueeze(1).to_broadcast([P, n, OUT]),
                 op=ADD,
             )
-            tiles = slice(j * QUAD, (j + 1) * QUAD)
             if j == QUADS - 1:
-                nc.sync.dma_start(out=out_view[:, tiles, cols], in_=o_sb_of[j][:, :, cols])
+                nc.sync.dma_start(out=out_view[:, j * QUAD + first : j * QUAD + first + n, cols], in_=o_sb_of[j][:, rows, cols])
             elif g == CODES - 1:
-                nc.sync.dma_start(out=out_view[:, tiles, :], in_=o_sb_of[j][:])
+                nc.sync.dma_start(out=out_view[:, j * QUAD : (j + 1) * QUAD, :], in_=o_sb_of[j][:])
 
         def live(k):
             return 0 <= k < UNITS
 
         with tc.manual_schedule():
-            for k in range(-2, UNITS + 3):
+            for k in range(-2, LAST):
                 if live(k - 2):
                     second_layer(k - 2)
                 if live(k):
@@ -243,14 +273,34 @@ def tile_linearwdecoder_pb_t_e_kernel(tc, h, W3_words, W3_scales, b3, Wo_words, 
                     sort_w3(0)
                 if live(k + 1):
                     h_q_of[k + 1] = quantise(h_t_of[k + 1], three, "h")
-                    first_layer(k + 1, [0, 1, 2])
-                if 0 < k + 2 < CODES:
-                    sort_w3(k + 2)
+                    first_layer(k + 1, [0, 1, 2, 3] if k + 1 == LAST else [0, 1, 2])
+                if k == -1:
+                    sort_w3(1)
+                if k == 0:
+                    sort_w3(2)
+                    sort_w3(3)
                 if live(k - 1):
-                    h3_q_of[k - 1] = quantise_h3(k - 1)
+                    quantise_h3(k - 1)
                 if live(k - 2):
                     bias_store(k - 2)
                 if live(k):
                     add_from_psum(k)
                     add_from_sbuf(nc.gpsimd, k, HALF, HALF + G_TOKENS)
                     add_from_sbuf(nc.vector, k, HALF + G_TOKENS, W)
+
+            second_layer(LAST - 2)
+            bias_relu_half(LAST, 0)
+            bias_relu_half(LAST, 1)
+            quantise_h3(LAST - 1)
+            bias_store(LAST - 2)
+            second_layer(LAST - 1)
+            add_from_psum(LAST)
+            bias_store(LAST - 1)
+            quantise_h3_half(LAST, 0)
+            second_layer(LAST, 0, 2)
+            add_from_sbuf(nc.gpsimd, LAST, HALF, HALF + G_TOKENS_LAST)
+            add_from_sbuf(nc.vector, LAST, HALF + G_TOKENS_LAST, W)
+            bias_store(LAST, 0, 2)
+            quantise_h3_half(LAST, 1)
+            second_layer(LAST, 2, 2, "tp_brief")
+            bias_store(LAST, 2, 2)

@@ -112,7 +112,7 @@ def tile_linearwdecoder_pb_t_e_kernel(tc, h, W3_words, W3_scales, b3, Wo_words, 
         def transpose_h(k):
             tp_kept = ps_three.tile([P, HALF, 2], F32, name="tp_kept")
             tp_brief = ps_one.tile([P, 2, HALF], F32, name="tp_brief")
-            for s in range(QUAD):
+            for s in (2, 3, 0, 1):
                 words = h_of[k][:, s, :].bitcast(F32)
                 for u in range(2):
                     if s < 2:
@@ -124,8 +124,8 @@ def tile_linearwdecoder_pb_t_e_kernel(tc, h, W3_words, W3_scales, b3, Wo_words, 
 
         def copy_h_t(k):
             h_t = four.tile([P, W, PACK], BF16, align_bytes=64, name="h_t")
-            nc.scalar.copy(out=h_t[:, 0:HALF, :].bitcast(F32), in_=tp_of[k][0][:])
             nc.scalar.copy(out=h_t[:, HALF:W, :].bitcast(F32), in_=tp_of[k][1][:].rearrange("p u w -> p w u"))
+            nc.scalar.copy(out=h_t[:, 0:HALF, :].bitcast(F32), in_=tp_of[k][0][:])
             h_t_of[k] = h_t
 
         def quantise(values, pool, name):

@@ -46,6 +46,7 @@ def tile_linearwdecoder_pb_t_e_kernel(tc, h, W3_words, W3_scales, b3, Wo_words, 
         one = stack.enter_context(tc.tile_pool(name="one", bufs=1))
         ps_one = stack.enter_context(tc.psum_pool(name="ps_one", bufs=1))
         ps_three = stack.enter_context(tc.psum_pool(name="ps_three", bufs=3))
+        ps_four = stack.enter_context(tc.psum_pool(name="ps_four", bufs=4))
 
         h_of = {}
 
@@ -111,7 +112,7 @@ def tile_linearwdecoder_pb_t_e_kernel(tc, h, W3_words, W3_scales, b3, Wo_words, 
 
         def transpose_h(k):
             tp_kept = ps_three.tile([P, HALF, 2], F32, name="tp_kept")
-            tp_brief = ps_one.tile([P, 2, HALF], F32, name="tp_brief")
+            tp_brief = ps_four.tile([P, 2, HALF], F32, name="short")
             for s in (2, 3, 0, 1):
                 words = h_of[k][:, s, :].bitcast(F32)
                 for u in range(2):
@@ -159,7 +160,7 @@ def tile_linearwdecoder_pb_t_e_kernel(tc, h, W3_words, W3_scales, b3, Wo_words, 
             x_of.setdefault(k, [])
             for t in ts:
                 cols = slice(t * P, (t + 1) * P)
-                x = ps_three.tile([P, W], F32, name="tp_kept" if (k == LAST and t == 3) else "x")
+                x = ps_four.tile([P, W], F32, name="short")
                 nc.tensor.matmul_mx(
                     out=x[:],
                     lhsT=w3_words[:, g, cols].bitcast(FP8X4),
@@ -222,7 +223,7 @@ def tile_linearwdecoder_pb_t_e_kernel(tc, h, W3_words, W3_scales, b3, Wo_words, 
         def second_layer(k, first=0, n=QUAD, bank="o"):
             g = k % CODES
             codes, scales = h3_q_of[k]
-            o = ps_one.tile([P, QUAD, OUT], F32, name=bank)
+            o = (ps_one if bank == "o" else ps_four).tile([P, QUAD, OUT], F32, name=bank)
             for s in range(first, first + n):
                 cols = slice(s * P, (s + 1) * P)
                 nc.tensor.matmul_mx(
@@ -261,9 +262,7 @@ def tile_linearwdecoder_pb_t_e_kernel(tc, h, W3_words, W3_scales, b3, Wo_words, 
                 if live(k - 2):
                     second_layer(k - 2)
                 if live(k):
-                    bias_relu(k, [0])
-                    first_layer(k, [3])
-                    bias_relu(k, [1, 2, 3])
+                    bias_relu(k, [0, 1, 2, 3])
                 if live(k + 2):
                     transpose_h(k + 2)
                     copy_h_t(k + 2)
@@ -273,7 +272,7 @@ def tile_linearwdecoder_pb_t_e_kernel(tc, h, W3_words, W3_scales, b3, Wo_words, 
                     sort_w3(0)
                 if live(k + 1):
                     h_q_of[k + 1] = quantise(h_t_of[k + 1], three, "h")
-                    first_layer(k + 1, [0, 1, 2, 3] if k + 1 == LAST else [0, 1, 2])
+                    first_layer(k + 1, [0, 1, 2, 3])
                 if k == -1:
                     sort_w3(1)
                 if k == 0:
@@ -302,5 +301,5 @@ def tile_linearwdecoder_pb_t_e_kernel(tc, h, W3_words, W3_scales, b3, Wo_words, 
             add_from_sbuf(nc.vector, LAST, HALF + G_TOKENS_LAST, W)
             bias_store(LAST, 0, 2)
             quantise_h3_half(LAST, 1)
-            second_layer(LAST, 2, 2, "tp_brief")
+            second_layer(LAST, 2, 2, "short")
             bias_store(LAST, 2, 2)

@@ -27,7 +27,7 @@ UNITS = QUADS * CODES
 H_BUFS = 12
 G_TOKENS = 168
 LAST = UNITS - 1
-G_TOKENS_LAST = 96
+G_TOKENS_LAST = 136
 
 FLOPS = 2 * TOKENS * CODES * HID * (HID + OUT)
 
@@ -53,7 +53,11 @@ def tile_linearwdecoder_pb_t_e_kernel(tc, h, W3_words, W3_scales, b3, Wo_words, 
         def load_h(k):
             j, g = divmod(k, CODES)
             h_unit = h_pool.tile([P, QUAD, HID], BF16, name="h_unit")
-            nc.sync.dma_start(out=h_unit[:], in_=h_view[:, j * QUAD : (j + 1) * QUAD, g * HID : (g + 1) * HID])
+            pieces = ((2, 4), (0, 2)) if k == 0 else ((0, QUAD),)
+            for a, b in pieces:
+                nc.sync.dma_start(
+                    out=h_unit[:, a:b, :], in_=h_view[:, j * QUAD + a : j * QUAD + b, g * HID : (g + 1) * HID]
+                )
             h_of[k] = h_unit
 
         w3_raw = keep.tile([P, CODES, HID], I32, align_bytes=64)
@@ -299,7 +303,11 @@ def tile_linearwdecoder_pb_t_e_kernel(tc, h, W3_words, W3_scales, b3, Wo_words, 
             second_layer(LAST, 0, 2)
             add_from_sbuf(nc.gpsimd, LAST, HALF, HALF + G_TOKENS_LAST)
             add_from_sbuf(nc.vector, LAST, HALF + G_TOKENS_LAST, W)
-            bias_store(LAST, 0, 2)
             quantise_h3_half(LAST, 1)
+            o_front = o_of[LAST]
             second_layer(LAST, 2, 2, "short")
+            o_back = o_of[LAST]
+            o_of[LAST] = o_front
+            bias_store(LAST, 0, 2)
+            o_of[LAST] = o_back
             bias_store(LAST, 2, 2)

@@ -53,7 +53,7 @@ def tile_linearwdecoder_pb_t_e_kernel(tc, h, W3_words, W3_scales, b3, Wo_words, 
         def load_h(k):
             j, g = divmod(k, CODES)
             h_unit = h_pool.tile([P, QUAD, HID], BF16, name="h_unit")
-            pieces = ((2, 4), (0, 2)) if k == 0 else ((0, QUAD),)
+            pieces = ((2, 4), (0, 2)) if k < 2 else ((0, QUAD),)
             for a, b in pieces:
                 nc.sync.dma_start(
                     out=h_unit[:, a:b, :], in_=h_view[:, j * QUAD + a : j * QUAD + b, g * HID : (g + 1) * HID]

from contextlib import ExitStack

from concourse import mybir
from concourse.masks import make_identity

F32 = mybir.dt.float32
BF16 = mybir.dt.bfloat16
I32 = mybir.dt.int32
U32 = mybir.dt.uint32
U8 = mybir.dt.uint8
FP8X4 = mybir.dt.float8_e4m3fn_x4
RELU = mybir.ActivationFunctionType.Relu
ADD = mybir.AluOpType.add

P = 128
PACK = 4
TOKENS = 4096
CODES = 4
HID = 512
OUT = 128
TILES = TOKENS // P
QUAD = 4
W = QUAD * P
HALF = W // 2
QUADS = TILES // QUAD
UNITS = QUADS * CODES
H_BUFS = 12
G_TOKENS = 168
LAST = UNITS - 1
G_TOKENS_LAST = 136

FLOPS = 2 * TOKENS * CODES * HID * (HID + OUT)


def tile_linearwdecoder_pb_t_e_kernel(tc, h, W3_words, W3_scales, b3, Wo_words, Wo_scales, bo, out):
    nc = tc.nc
    h_view = h.rearrange("(p i) g k -> p i (g k)", i=TILES)
    out_view = out.rearrange("(p i) n -> p i n", i=TILES)

    with ExitStack() as stack:
        keep = stack.enter_context(tc.tile_pool(name="keep", bufs=1))
        h_pool = stack.enter_context(tc.tile_pool(name="h_pool", bufs=H_BUFS))
        two = stack.enter_context(tc.tile_pool(name="two", bufs=2))
        three = stack.enter_context(tc.tile_pool(name="three", bufs=3))
        four = stack.enter_context(tc.tile_pool(name="four", bufs=4))
        one = stack.enter_context(tc.tile_pool(name="one", bufs=1))
        ps_one = stack.enter_context(tc.psum_pool(name="ps_one", bufs=1))
        ps_three = stack.enter_context(tc.psum_pool(name="ps_three", bufs=3))
        ps_four = stack.enter_context(tc.psum_pool(name="ps_four", bufs=4))

        h_of = {}

        def load_h(k):
            j, g = divmod(k, CODES)
            h_unit = h_pool.tile([P, QUAD, HID], BF16, name="h_unit")
            pieces = ((2, 4), (0, 2)) if k < 2 else ((0, QUAD),)
            for a, b in pieces:
                nc.sync.dma_start(
                    out=h_unit[:, a:b, :], in_=h_view[:, j * QUAD + a : j * QUAD + b, g * HID : (g + 1) * HID]
                )
            h_of[k] = h_unit

        w3_raw = keep.tile([P, CODES, HID], I32, align_bytes=64)
        w3_scales_raw = keep.tile([P, CODES, HID], U8, align_bytes=64)
        wo_scales = keep.tile([P, CODES, OUT], U8, align_bytes=64)
        nc.vector.memset(w3_scales_raw[:].rearrange("p g n -> p (g n)").bitcast(I32), 0)
        nc.vector.memset(wo_scales[:].rearrange("p g n -> p (g n)").bitcast(I32), 0)

        def load_scales(tile, scales):
            for quad in range(4):
                nc.sync.dma_start(
                    out=tile[32 * quad : 32 * quad + 4, :, :].bitcast(I32),
                    in_=scales[:, 4 * quad : 4 * quad + 4, :].rearrange("g r n -> r g n").bitcast(I32),
                )

        load_scales(w3_scales_raw, W3_scales)
        def load_w3(g):
            nc.sync.dma_start(out=w3_raw[:, g, :], in_=W3_words[g].rearrange("p n t -> p (n t)").bitcast(I32))

        load_h(0)
        load_w3(0)
        load_h(1)
        load_w3(1)
        load_w3(2)
        load_w3(3)
        load_h(2)
        load_h(3)
        load_scales(wo_scales, Wo_scales)
        wo_words = keep.tile([P, CODES, OUT], I32, align_bytes=64)
        nc.sync.dma_start(out=wo_words[:], in_=Wo_words.rearrange("g p n t -> p g (n t)").bitcast(I32))
        bo_row = keep.tile([P, CODES * OUT], BF16)
        nc.sync.dma_start(out=bo_row[:], in_=bo.rearrange("g o -> (g o)").partition_broadcast(P))
        for k in range(CODES, H_BUFS):
            load_h(k)

        ident = keep.tile([P, P], F32)
        make_identity(nc, ident[:])

        b3_cols = keep.tile([P, CODES, PACK], BF16)
        nc.scalar.dma_start(out=b3_cols[:], in_=b3.rearrange("g (p t) -> p g t", t=PACK))
        w3_words = keep.tile([P, CODES, HID], I32, align_bytes=64)
        w3_scales = keep.tile([P, CODES, HID], U8, align_bytes=64)

        def sort_w3(g):
            nc.vector.tensor_copy(
                out=w3_scales[:, g, :].rearrange("p (t m) -> p m t", t=PACK),
                in_=w3_scales_raw[:, g, :].rearrange("p (m t) -> p m t", t=PACK),
            )
            nc.vector.tensor_copy(
                out=w3_words[:, g, :].rearrange("p (t m) -> p t m", t=PACK),
                in_=w3_raw[:, g, :].rearrange("p (m t) -> p t m", t=PACK),
            )

        tp_of, h_t_of, h_q_of, x_of, r_of, h3_t_of, h3_q_of, o_of, o_sb_of = ({}, {}, {}, {}, {}, {}, {}, {}, {})
        r_whole_of = {}

        def transpose_h(k):
            tp_kept = ps_three.tile([P, HALF, 2], F32, name="tp_kept")
            tp_brief = ps_four.tile([P, 2, HALF], F32, name="short")
            for s in (2, 3, 0, 1):
                words = h_of[k][:, s, :].bitcast(F32)
                for u in range(2):
                    if s < 2:
                        dest = tp_kept[:, s * P : (s + 1) * P, u]
                    else:
                        dest = tp_brief[:, u, (s - 2) * P : (s - 1) * P]
                    nc.tensor.transpose(dest, words[:, u : HID // 2 : 2], ident[:])
            tp_of[k] = [tp_kept, tp_brief]

        def copy_h_t(k):
            h_t = four.tile([P, W, PACK], BF16, align_bytes=64, name="h_t")
            nc.scalar.copy(out=h_t[:, HALF:W, :].bitcast(F32), in_=tp_of[k][1][:].rearrange("p u w -> p w u"))
            nc.scalar.copy(out=h_t[:, 0:HALF, :].bitcast(F32), in_=tp_of[k][0][:])
            h_t_of[k] = h_t

        def quantise(values, pool, name):
            codes = pool.tile([P, W], U32, align_bytes=64, name=name + "_codes")
            scales = pool.tile([P, W], U8, align_bytes=64, name=name + "_scales")
            nc.vector.quantize_mx(
                out=codes[:].bitcast(FP8X4), scales=scales[:], in_=values[:].rearrange("p w t -> p (w t)")
            )
            return codes, scales

        def quantise_h3_half(k, a):
            if k not in h3_q_of:
                codes = two.tile([P, W], U32, align_bytes=64, name="h3_codes")
                scales = two.tile([P, W], U8, align_bytes=64, name="h3_scales")
                h3_q_of[k] = (codes, scales)
            codes, scales = h3_q_of[k]
            cols = slice(a * HALF, (a + 1) * HALF)
            nc.vector.quantize_mx(
                out=codes[:, cols].bitcast(FP8X4),
                scales=scales[:, cols],
                in_=h3_t_of[k][a][:].rearrange("p w t -> p (w t)"),
            )

        def quantise_h3(k):
            quantise_h3_half(k, 1)
            quantise_h3_half(k, 0)

        def first_layer(k, ts):
            g = k % CODES
            codes, scales = h_q_of[k]
            x_of.setdefault(k, [])
            for t in ts:
                cols = slice(t * P, (t + 1) * P)
                x = ps_four.tile([P, W], F32, name="short")
                nc.tensor.matmul_mx(
                    out=x[:],
                    lhsT=w3_words[:, g, cols].bitcast(FP8X4),
                    lhsT_scale=w3_scales[:, g, cols],
                    rhs=codes[:].bitcast(FP8X4),
                    rhs_scale=scales[:],
                    start=True,
                    stop=True,
                )
                x_of[k].append(x)

        def bias_relu(k, ts):
            g = k % CODES
            if k not in r_whole_of:
                r_whole_of[k] = three.tile([P, PACK, W], F32, name="r")
                r_of[k] = [r_whole_of[k][:, :, 0:HALF], r_whole_of[k][:, :, HALF:W]]
            r = r_whole_of[k]
            for t in ts:
                nc.scalar.activation(
                    out=r[:, t, :],
                    in_=x_of[k][t][:],
                    func=RELU,
                    bias=b3_cols[:, g, t : t + 1],
                    scale=1.0,
                )

        def bias_relu_half(k, a):
            g = k % CODES
            r_half = one.tile([P, PACK, HALF], F32, name="r_half%d" % a)
            for t in range(PACK):
                nc.scalar.activation(
                    out=r_half[:, t, :],
                    in_=x_of[k][t][:, a * HALF : (a + 1) * HALF],
                    func=RELU,
                    bias=b3_cols[:, g, t : t + 1],
                    scale=1.0,
                )
            r_of.setdefault(k, []).append(r_half[:])

        def add_from_psum(k):
            h3_front = one.tile([P, HALF, PACK], BF16, align_bytes=64, name="h3_front")
            h3_back = one.tile([P, HALF, PACK], BF16, align_bytes=64, name="h3_back")
            nc.vector.tensor_tensor(
                out=h3_front[:].rearrange("p (c i) t -> p c t i", i=4),
                in0=tp_of[k][0][:].bitcast(BF16).rearrange("p (c i) t -> p c t i", i=4),
                in1=r_of[k][0].rearrange("p t (c i) -> p c t i", i=4),
                op=ADD,
            )
            h3_t_of[k] = [h3_front, h3_back]

        def add_from_sbuf(engine, k, first, last):
            tokens = slice(first, last)
            engine.tensor_tensor(
                out=h3_t_of[k][1][:, first - HALF : last - HALF, :].rearrange("p (c i) t -> p c t i", i=4),
                in0=r_of[k][1][:, :, first - HALF : last - HALF].rearrange("p t (c i) -> p c t i", i=4),
                in1=h_t_of[k][:, tokens, :].rearrange("p (c i) t -> p c t i", i=4),
                op=ADD,
            )

        def second_layer(k, first=0, n=QUAD, bank="o"):
            g = k % CODES
            codes, scales = h3_q_of[k]
            o = (ps_one if bank == "o" else ps_four).tile([P, QUAD, OUT], F32, name=bank)
            for s in range(first, first + n):
                cols = slice(s * P, (s + 1) * P)
                nc.tensor.matmul_mx(
                    out=o[:, s, :],
                    lhsT=codes[:, cols].bitcast(FP8X4),
                    lhsT_scale=scales[:, cols],
                    rhs=wo_words[:, g, :].bitcast(FP8X4),
                    rhs_scale=wo_scales[:, g, :],
                    start=True,
                    stop=True,
                )
            o_of[k] = o

        def bias_store(k, first=0, n=QUAD):
            j, g = divmod(k, CODES)
            if j not in o_sb_of:
                o_sb_of[j] = two.tile([P, QUAD, CODES * OUT], F32, name="o_sb")
            cols = slice(g * OUT, (g + 1) * OUT)
            rows = slice(first, first + n)
            nc.vector.tensor_tensor(
                out=o_sb_of[j][:, rows, cols],
                in0=o_of[k][:, rows, :],
                in1=bo_row[:, cols].unsqueeze(1).to_broadcast([P, n, OUT]),
                op=ADD,
            )
            if j == QUADS - 1:
                nc.sync.dma_start(out=out_view[:, j * QUAD + first : j * QUAD + first + n, cols], in_=o_sb_of[j][:, rows, cols])
            elif g == CODES - 1:
                nc.sync.dma_start(out=out_view[:, j * QUAD : (j + 1) * QUAD, :], in_=o_sb_of[j][:])

        def live(k):
            return 0 <= k < UNITS

        with tc.manual_schedule():
            for k in range(-2, LAST):
                if live(k - 2):
                    second_layer(k - 2)
                if live(k):
                    bias_relu(k, [0, 1, 2, 3])
                if live(k + 2):
                    transpose_h(k + 2)
                    copy_h_t(k + 2)
                    if live(k + 2 + H_BUFS):
                        load_h(k + 2 + H_BUFS)
                if k + 2 == 0:
                    sort_w3(0)
                if live(k + 1):
                    h_q_of[k + 1] = quantise(h_t_of[k + 1], three, "h")
                    first_layer(k + 1, [0, 1, 2, 3])
                if k == -1:
                    sort_w3(1)
                if k == 0:
                    sort_w3(2)
                    sort_w3(3)
                if live(k - 1):
                    quantise_h3(k - 1)
                if live(k - 2):
                    bias_store(k - 2)
                if live(k):
                    add_from_psum(k)
                    add_from_sbuf(nc.gpsimd, k, HALF, HALF + G_TOKENS)
                    add_from_sbuf(nc.vector, k, HALF + G_TOKENS, W)

            second_layer(LAST - 2)
            bias_relu_half(LAST, 0)
            bias_relu_half(LAST, 1)
            quantise_h3(LAST - 1)
            bias_store(LAST - 2)
            second_layer(LAST - 1)
            add_from_psum(LAST)
            bias_store(LAST - 1)
            quantise_h3_half(LAST, 0)
            second_layer(LAST, 0, 2)
            add_from_sbuf(nc.gpsimd, LAST, HALF, HALF + G_TOKENS_LAST)
            add_from_sbuf(nc.vector, LAST, HALF + G_TOKENS_LAST, W)
            quantise_h3_half(LAST, 1)
            o_front = o_of[LAST]
            second_layer(LAST, 2, 2, "short")
            o_back = o_of[LAST]
            o_of[LAST] = o_front
            bias_store(LAST, 0, 2)
            o_of[LAST] = o_back
            bias_store(LAST, 2, 2)
